import numpy as np
import ml_dtypes


def mxq(x, axis, fmt="e4m3"):
    dtype, down = {"e4m3": (ml_dtypes.float8_e4m3fn, 7), "e5m2": (ml_dtypes.float8_e5m2, 14)}[fmt]
    v = np.moveaxis(np.asarray(x, np.float32).astype(ml_dtypes.bfloat16).astype(np.float64), axis, -1)
    blocks = v.reshape(v.shape[:-1] + (-1, 32))
    amax = np.abs(blocks).max(-1, keepdims=True)
    byte = np.maximum(np.where(amax > 0, np.frexp(amax)[1] - 1 + 127, 0) - down, 1)
    scale = np.exp2(byte - 127.0)
    codes = (blocks / scale).astype(np.float32).astype(dtype).astype(np.float64)
    return np.moveaxis((codes * scale).reshape(v.shape), -1, axis)


WIDE = False


def mx_kscale(k):
    if not WIDE:
        return np.ones(k)
    levels = np.array([10, -10, 5, -5, 0])
    if k % 512:
        return np.exp2(np.random.permutation(np.resize(levels, k // 32))).repeat(32)
    a = np.empty((k // 512, 16))
    for p in range(k // 512):
        a[p, :8] = np.random.permutation(np.resize(levels, 8))
        for g in range(8):
            far = levels[np.abs(levels - a[p, g]) >= 10]
            a[p, g + 8] = far[np.random.randint(len(far))]
    return np.exp2(a.ravel()).repeat(32)


BF16 = ml_dtypes.bfloat16


def bf(x):
    return np.asarray(x, np.float32).astype(BF16)


def f64(x):
    return np.asarray(x).astype(np.float64)


B, C, HH, WW, NH = 4, 512, 32, 32, 8
N = HH * WW
DH = C // NH
HALF = C // 2


def pos_encoding():
    positions = np.arange(N, dtype=np.float64)
    depths = np.arange(HALF, dtype=np.float64) / HALF
    angle_rates = 1.0 / (10000.0 ** depths)
    angle_rads = positions[:, None] * angle_rates[None, :]
    return np.concatenate([np.sin(angle_rads), np.cos(angle_rads)], axis=-1)


def heads(t):
    return t.reshape(B, N, NH, DH).transpose(0, 2, 1, 3)


def setup_inputs():
    bound = np.sqrt(6.0 / (C + 3 * C))
    s = mx_kscale(C)
    u = s / s.min()
    return {"x": bf(np.random.standard_normal((B, C, HH, WW)) * u[None, :, None, None]),
            "W_qkv": bf(np.random.uniform(-bound, bound, (3 * C, C)) / u[None, :])}


def reference(x, W_qkv):
    xt = f64(x).reshape(B, C, N) + pos_encoding().T[None]
    tokens = xt.transpose(0, 2, 1)
    qkv = mxq(tokens, 2, "e4m3") @ mxq(f64(W_qkv), 1, "e4m3").T
    q, k, v = np.split(qkv, 3, axis=-1)
    return heads(q), heads(k), heads(v)

@@ -1,0 +1,268 @@
+import math
+from contextlib import ExitStack
+
+import concourse.mybir as mybir
+from concourse.masks import make_identity
+
+F32 = mybir.dt.float32
+BF16 = mybir.dt.bfloat16
+U32 = mybir.dt.uint32
+U8 = mybir.dt.uint8
+FP8X4 = mybir.dt.float8_e4m3fn_x4
+ALU = mybir.AluOpType
+ACT = mybir.ActivationFunctionType
+
+P = 128
+PACK = 4
+BATCH = 4
+CHANNELS = 512
+POSITIONS = 1024
+HEADS = 8
+HEAD_DIM = 64
+OUT_COLS = HEADS * HEAD_DIM
+RUN = 8
+HALF_RUN = RUN // 2
+GROUPS = POSITIONS // RUN
+HALF_COLS = GROUPS * HALF_RUN
+ROUND_MAGIC = 12582912.0
+
+FLOPS = 2 * BATCH * POSITIONS * CHANNELS * 3 * OUT_COLS
+
+
+def tile_multiheadselfattention_pa_t_kernel(tc, x, W_qkv, out_0, out_1, out_2):
+    nc = tc.nc
+    outs = [out_0, out_1, out_2]
+    with ExitStack() as ctx:
+        const = ctx.enter_context(tc.tile_pool(name="const", bufs=1))
+        angles = ctx.enter_context(tc.tile_pool(name="angles", bufs=4))
+        tokens = ctx.enter_context(tc.tile_pool(name="tokens", bufs=2))
+        staging = ctx.enter_context(tc.tile_pool(name="staging", bufs=5))
+        psum = ctx.enter_context(tc.psum_pool(name="psum", bufs=8))
+        ctx.enter_context(tc.manual_schedule())
+
+        w_raw = const.tile([P, 12, CHANNELS], BF16)
+        x_raw = [const.tile([P, PACK, POSITIONS], BF16, name="x_raw%d" % b) for b in range(BATCH)]
+
+        def load_w(g):
+            nc.sync.dma_start(
+                out=w_raw[:, 4 * g : 4 * g + 4, :],
+                in_=W_qkv[OUT_COLS * g : OUT_COLS * (g + 1), :].rearrange("(a o) k -> o a k", o=P),
+            )
+
+        def load_x(b):
+            nc.sync.dma_start(
+                out=x_raw[b][:],
+                in_=x[b].rearrange("c h w -> c (h w)").rearrange("(q j) n -> q j n", j=PACK),
+            )
+
+        load_w(0)
+        load_x(0)
+        load_w(1)
+        load_w(2)
+        for b in range(1, BATCH):
+            load_x(b)
+
+        zero = const.tile([P, 1], F32)
+        nc.vector.memset(zero[:], 0.0)
+        ten_thousand = const.tile([P, PACK], F32)
+        nc.vector.memset(ten_thousand[:], 10000.0)
+        warm = const.tile([P, 1], F32)
+        nc.scalar.activation(out=warm[:], in_=zero[:], func=ACT.Sin)
+
+        count = const.tile([P, GROUPS], F32)
+        nc.gpsimd.iota(
+            count[:], pattern=[[1, GROUPS]], base=0, channel_multiplier=0,
+            allow_small_or_imprecise_dtypes=True,
+        )
+        position = const.tile([P, 2, GROUPS, HALF_RUN], F32)
+        for s in range(2):
+            nc.vector.scalar_tensor_tensor(
+                out=position[:, s, :, :],
+                in0=count[:].unsqueeze(2).to_broadcast([P, GROUPS, HALF_RUN]),
+                scalar=float(RUN),
+                in1=count[:, HALF_RUN * s : HALF_RUN * (s + 1)]
+                .unsqueeze(1)
+                .to_broadcast([P, GROUPS, HALF_RUN]),
+                op0=ALU.mult,
+                op1=ALU.add,
+            )
+
+        channel = const.tile([P, PACK], F32)
+        nc.gpsimd.iota(
+            channel[:], pattern=[[1, PACK]], base=0, channel_multiplier=PACK,
+            allow_small_or_imprecise_dtypes=True,
+        )
+        phase = const.tile([P, PACK], F32)
+        nc.vector.tensor_scalar(
+            out=phase[:], in0=channel[:], scalar1=256.0, scalar2=0.25, op0=ALU.is_ge, op1=ALU.mult
+        )
+        depth = const.tile([P, PACK], F32)
+        nc.vector.tensor_scalar(
+            out=depth[:], in0=channel[:], scalar1=-1.0 / 256.0, scalar2=None, op0=ALU.mult
+        )
+        exponent = const.tile([P, PACK], F32)
+        nc.vector.scalar_tensor_tensor(
+            out=exponent[:], in0=phase[:], scalar=4.0, in1=depth[:], op0=ALU.mult, op1=ALU.add
+        )
+        radians = const.tile([P, PACK], F32)
+        nc.gpsimd.tensor_tensor(out=radians[:], in0=ten_thousand[:], in1=exponent[:], op=ALU.pow)
+        rate = const.tile([P, PACK], F32)
+        nc.vector.tensor_scalar(
+            out=rate[:], in0=radians[:], scalar1=1.0 / (2.0 * math.pi), scalar2=None, op0=ALU.mult
+        )
+
+        identity = const.tile([P, P], F32)
+        make_identity(nc, identity[:])
+
+        w_grouped = const.tile([P, 3 * OUT_COLS * PACK], BF16, align_bytes=64)
+        w_words = w_grouped[:].bitcast(F32).rearrange("q (o u) -> q o u", u=2)
+        w_codes = const.tile([P, 3 * OUT_COLS], U32, align_bytes=64)
+        w_scales = const.tile([P, 3 * OUT_COLS], U8, align_bytes=64)
+        flipped = {}
+
+        def flip_w(g):
+            for pair in range(2 * g, 2 * g + 2):
+                flipped[pair] = psum.tile([P, 2, 2, P], F32, name="flipped", tag="bank")
+                for a in range(2):
+                    words = w_raw[:, 2 * pair + a, :].bitcast(F32)
+                    for u in range(2):
+                        nc.tensor.transpose(
+                            flipped[pair][:, a, u, :], words[:, u :: 2], identity[:]
+                        )
+
+        def regroup_w(g):
+            for pair in range(2 * g, 2 * g + 2):
+                dst = w_words[:, 2 * P * pair : 2 * P * (pair + 1), :].rearrange(
+                    "q (a o) u -> q a o u", a=2
+                )
+                src = flipped[pair][:].rearrange("q a u o -> q a o u")
+                if g % 2 == 0:
+                    nc.scalar.copy(out=dst, in_=src)
+                else:
+                    nc.vector.tensor_copy(out=dst, in_=src)
+
+        def quantise_w(g):
+            cols = slice(OUT_COLS * g, OUT_COLS * (g + 1))
+            nc.vector.quantize_mx(
+                out=w_codes[:, cols].bitcast(FP8X4),
+                scales=w_scales[:, cols],
+                in_=w_grouped[:, PACK * OUT_COLS * g : PACK * OUT_COLS * (g + 1)],
+            )
+
+        pe = [const.tile([P, PACK, HALF_COLS], F32, name="pe%d" % s) for s in range(2)]
+
+        def make_table(s, j):
+            angle = angles.tile([P, HALF_COLS], F32)
+            nc.vector.tensor_scalar(
+                out=angle[:], in0=position[:, s, :, :].rearrange("q m t -> q (m t)"),
+                scalar1=rate[:, j : j + 1], scalar2=phase[:, j : j + 1], op0=ALU.mult, op1=ALU.add,
+            )
+            whole = angles.tile([P, HALF_COLS], F32)
+            nc.vector.tensor_scalar(
+                out=whole[:], in0=angle[:], scalar1=ROUND_MAGIC, scalar2=None, op0=ALU.add
+            )
+            back = angles.tile([P, HALF_COLS], F32)
+            nc.vector.scalar_tensor_tensor(
+                out=back[:], in0=whole[:], scalar=ROUND_MAGIC, in1=angle[:],
+                op0=ALU.subtract, op1=ALU.subtract,
+            )
+            nc.scalar.activation(out=pe[s][:, j, :], in_=back[:], func=ACT.Sin, scale=-2.0 * math.pi)
+
+        token_tiles = {}
+
+        def add_table(b, s):
+            if s == 0:
+                token_tiles[b] = (
+                    tokens.tile([P, RUN, GROUPS, PACK], BF16, name="grouped", align_bytes=64),
+                    tokens.tile([P, RUN, GROUPS], U32, name="codes", align_bytes=64),
+                    tokens.tile([P, RUN, GROUPS], U8, name="scales", align_bytes=64),
+                )
+            grouped = token_tiles[b][0]
+            half = slice(HALF_RUN * s, HALF_RUN * (s + 1))
+            nc.vector.tensor_tensor(
+                out=grouped[:, half, :, :].rearrange("q t m j -> q m j t"),
+                in0=x_raw[b][:].rearrange("q j (m s t) -> q s m j t", s=2, t=HALF_RUN)[:, s],
+                in1=pe[s][:].rearrange("q j (m t) -> q m j t", t=HALF_RUN),
+                op=ALU.add,
+            )
+
+        def quantise_tokens(b, s):
+            grouped, codes, scales = token_tiles[b]
+            half = slice(HALF_RUN * s, HALF_RUN * (s + 1))
+            nc.vector.quantize_mx(
+                out=codes[:, half, :].rearrange("q t m -> q (t m)").bitcast(FP8X4),
+                scales=scales[:, half, :].rearrange("q t m -> q (t m)"),
+                in_=grouped[:, half, :, :].rearrange("q t m j -> q (t m j)"),
+            )
+
+        def prepare_tokens(b, step):
+            if step < 2:
+                add_table(b, step)
+            if step > 0:
+                quantise_tokens(b, step - 1)
+
+        stage_tiles = {}
+
+        def project(b, g, s):
+            codes, scales = token_tiles[b][1], token_tiles[b][2]
+            cols = slice(OUT_COLS * g, OUT_COLS * (g + 1))
+            if s == 0:
+                stage_tiles[(b, g)] = staging.tile([P, HEADS, RUN, HEAD_DIM], F32, name="stage")
+            stage = stage_tiles[(b, g)]
+            for t in range(HALF_RUN * s, HALF_RUN * (s + 1)):
+                acc = psum.tile([P, OUT_COLS], F32, tag="bank")
+                nc.tensor.matmul_mx(
+                    out=acc[:],
+                    lhsT=codes[:, t, :].bitcast(FP8X4),
+                    lhsT_scale=scales[:, t, :],
+                    rhs=w_codes[:, cols].bitcast(FP8X4),
+                    rhs_scale=w_scales[:, cols],
+                    start=True,
+                    stop=True,
+                )
+                by_head = acc[:].rearrange("m (h d) -> m h d", d=HEAD_DIM)
+                if t % 4 == 3:
+                    nc.vector.tensor_copy(out=stage[:, :, t, :], in_=by_head)
+                else:
+                    nc.scalar.copy(out=stage[:, :, t, :], in_=by_head)
+
+        def store(b, g, part, parts):
+            nc.sync.dma_start(
+                out=outs[g][b].rearrange("h (m c r) d -> c m h (r d)", c=parts, r=RUN // parts)[part],
+                in_=stage_tiles[(b, g)][:].rearrange("m h (c r) d -> m c h (r d)", c=parts)[:, part],
+            )
+
+        for j in range(PACK):
+            make_table(0, j)
+        flip_w(0)
+        flip_w(1)
+        regroup_w(0)
+        for j in range(PACK):
+            make_table(1, j)
+        flip_w(2)
+        add_table(0, 0)
+        quantise_w(0)
+        quantise_tokens(0, 0)
+        regroup_w(1)
+        quantise_w(1)
+        project(0, 0, 0)
+        store(0, 0, 0, 2)
+        regroup_w(2)
+        add_table(0, 1)
+        quantise_w(2)
+        quantise_tokens(0, 1)
+        for g in range(1, 3):
+            project(0, g, 0)
+            store(0, g, 0, 2)
+        for g in range(3):
+            project(0, g, 1)
+            store(0, g, 1, 2)
+            prepare_tokens(1, g)
+
+        for b in range(1, BATCH):
+            for g in range(3):
+                project(b, g, 0)
+                project(b, g, 1)
+                store(b, g, 0, 1)
+                if b + 1 < BATCH:
+                    prepare_tokens(b + 1, g)

@@ -20,13 +20,17 @@ POSITIONS = 1024
 HEADS = 8
 HEAD_DIM = 64
 OUT_COLS = HEADS * HEAD_DIM
-RUN = 8
-HALF_RUN = RUN // 2
-GROUPS = POSITIONS // RUN
-HALF_COLS = GROUPS * HALF_RUN
+THIRDS = 3
+PAIR = 2
+PAIRS = BATCH // PAIR
+ROWS = P // PAIR
+RUN = POSITIONS // ROWS
+STEP = 4
+STEPS = RUN // STEP
+STEP_COLS = ROWS * STEP
 ROUND_MAGIC = 12582912.0
 
-FLOPS = 2 * BATCH * POSITIONS * CHANNELS * 3 * OUT_COLS
+FLOPS = 2 * BATCH * POSITIONS * CHANNELS * THIRDS * OUT_COLS
 
 
 def tile_multiheadselfattention_pa_t_kernel(tc, x, W_qkv, out_0, out_1, out_2):
@@ -34,112 +38,107 @@ def tile_multiheadselfattention_pa_t_kernel(tc, x, W_qkv, out_0, out_1, out_2):
     outs = [out_0, out_1, out_2]
     with ExitStack() as ctx:
         const = ctx.enter_context(tc.tile_pool(name="const", bufs=1))
-        angles = ctx.enter_context(tc.tile_pool(name="angles", bufs=4))
+        angle_pool = ctx.enter_context(tc.tile_pool(name="angle_pool", bufs=3))
+        turn_pool = ctx.enter_context(tc.tile_pool(name="turn_pool", bufs=2))
         tokens = ctx.enter_context(tc.tile_pool(name="tokens", bufs=2))
-        staging = ctx.enter_context(tc.tile_pool(name="staging", bufs=5))
+        grouping = ctx.enter_context(tc.tile_pool(name="grouping", bufs=3))
+        staging = ctx.enter_context(tc.tile_pool(name="staging", bufs=3))
         psum = ctx.enter_context(tc.psum_pool(name="psum", bufs=8))
         ctx.enter_context(tc.manual_schedule())
 
-        w_raw = const.tile([P, 12, CHANNELS], BF16)
-        x_raw = [const.tile([P, PACK, POSITIONS], BF16, name="x_raw%d" % b) for b in range(BATCH)]
+        w_raw = const.tile([P, THIRDS, 4, CHANNELS], BF16)
+        x_raw = [const.tile([P, PAIR, PACK, POSITIONS], BF16, name="x_raw%d" % i) for i in range(PAIRS)]
 
         def load_w(g):
             nc.sync.dma_start(
-                out=w_raw[:, 4 * g : 4 * g + 4, :],
-                in_=W_qkv[OUT_COLS * g : OUT_COLS * (g + 1), :].rearrange("(a o) k -> o a k", o=P),
+                out=w_raw[:, g, :, :],
+                in_=W_qkv[OUT_COLS * g : OUT_COLS * (g + 1), :].rearrange("(m t) k -> m t k", t=4),
             )
 
         def load_x(b):
             nc.sync.dma_start(
-                out=x_raw[b][:],
+                out=x_raw[b // PAIR][:, b % PAIR, :, :],
                 in_=x[b].rearrange("c h w -> c (h w)").rearrange("(q j) n -> q j n", j=PACK),
             )
 
         load_w(0)
         load_x(0)
+        load_x(1)
         load_w(1)
         load_w(2)
-        for b in range(1, BATCH):
-            load_x(b)
+        load_x(2)
+        load_x(3)
 
         zero = const.tile([P, 1], F32)
         nc.vector.memset(zero[:], 0.0)
-        ten_thousand = const.tile([P, PACK], F32)
-        nc.vector.memset(ten_thousand[:], 10000.0)
         warm = const.tile([P, 1], F32)
         nc.scalar.activation(out=warm[:], in_=zero[:], func=ACT.Sin)
-
-        count = const.tile([P, GROUPS], F32)
-        nc.gpsimd.iota(
-            count[:], pattern=[[1, GROUPS]], base=0, channel_multiplier=0,
-            allow_small_or_imprecise_dtypes=True,
-        )
-        position = const.tile([P, 2, GROUPS, HALF_RUN], F32)
-        for s in range(2):
-            nc.vector.scalar_tensor_tensor(
-                out=position[:, s, :, :],
-                in0=count[:].unsqueeze(2).to_broadcast([P, GROUPS, HALF_RUN]),
-                scalar=float(RUN),
-                in1=count[:, HALF_RUN * s : HALF_RUN * (s + 1)]
-                .unsqueeze(1)
-                .to_broadcast([P, GROUPS, HALF_RUN]),
-                op0=ALU.mult,
-                op1=ALU.add,
-            )
 
         channel = const.tile([P, PACK], F32)
         nc.gpsimd.iota(
             channel[:], pattern=[[1, PACK]], base=0, channel_multiplier=PACK,
             allow_small_or_imprecise_dtypes=True,
         )
+        depth = const.tile([P, PACK], F32)
+        nc.gpsimd.tensor_scalar(
+            out=depth[:], in0=channel[:], scalar1=-1.0 / 256.0, scalar2=0.0, op0=ALU.mult, op1=ALU.add
+        )
+        ten_thousand = const.tile([P, PACK], F32)
+        nc.vector.memset(ten_thousand[:], 10000.0)
+        position = const.tile([P, ROWS, STEP], F32)
+        nc.gpsimd.iota(
+            position[:], pattern=[[RUN, ROWS], [1, STEP]], base=0, channel_multiplier=0,
+            allow_small_or_imprecise_dtypes=True,
+        )
+        power = const.tile([P, PACK], F32)
+        nc.gpsimd.tensor_tensor(out=power[:], in0=ten_thousand[:], in1=depth[:], op=ALU.pow)
+        identity = const.tile([P, P], F32)
+        make_identity(nc, identity[:])
         phase = const.tile([P, PACK], F32)
         nc.vector.tensor_scalar(
             out=phase[:], in0=channel[:], scalar1=256.0, scalar2=0.25, op0=ALU.is_ge, op1=ALU.mult
         )
-        depth = const.tile([P, PACK], F32)
+        beyond = const.tile([P, PACK], F32)
         nc.vector.tensor_scalar(
-            out=depth[:], in0=channel[:], scalar1=-1.0 / 256.0, scalar2=None, op0=ALU.mult
+            out=beyond[:], in0=channel[:], scalar1=256.0, scalar2=9999.0, op0=ALU.is_ge, op1=ALU.mult
         )
-        exponent = const.tile([P, PACK], F32)
-        nc.vector.scalar_tensor_tensor(
-            out=exponent[:], in0=phase[:], scalar=4.0, in1=depth[:], op0=ALU.mult, op1=ALU.add
-        )
-        radians = const.tile([P, PACK], F32)
-        nc.gpsimd.tensor_tensor(out=radians[:], in0=ten_thousand[:], in1=exponent[:], op=ALU.pow)
+        lift = const.tile([P, PACK], F32)
+        nc.vector.tensor_scalar(out=lift[:], in0=beyond[:], scalar1=1.0, scalar2=None, op0=ALU.add)
         rate = const.tile([P, PACK], F32)
         nc.vector.tensor_scalar(
-            out=rate[:], in0=radians[:], scalar1=1.0 / (2.0 * math.pi), scalar2=None, op0=ALU.mult
+            out=rate[:], in0=power[:], scalar1=lift[:, 0:1], scalar2=1.0 / (2.0 * math.pi),
+            op0=ALU.mult, op1=ALU.mult,
         )
+        start = const.tile([P, STEPS - 1, PACK], F32)
 
-        identity = const.tile([P, P], F32)
-        make_identity(nc, identity[:])
+        def make_start(c):
+            nc.vector.scalar_tensor_tensor(
+                out=start[:, c - 1, :], in0=rate[:], scalar=float(STEP * c), in1=phase[:],
+                op0=ALU.mult, op1=ALU.add,
+            )
 
-        w_grouped = const.tile([P, 3 * OUT_COLS * PACK], BF16, align_bytes=64)
-        w_words = w_grouped[:].bitcast(F32).rearrange("q (o u) -> q o u", u=2)
-        w_codes = const.tile([P, 3 * OUT_COLS], U32, align_bytes=64)
-        w_scales = const.tile([P, 3 * OUT_COLS], U8, align_bytes=64)
+        w_grouped = const.tile([P, THIRDS * OUT_COLS * PACK], BF16, align_bytes=64)
+        w_words = w_grouped[:].bitcast(F32).rearrange("q (g m t u) -> q g m t u", g=THIRDS, t=4, u=2)
+        w_codes = const.tile([P, THIRDS * OUT_COLS], U32, align_bytes=64)
+        w_scales = const.tile([P, THIRDS * OUT_COLS], U8, align_bytes=64)
         flipped = {}
 
         def flip_w(g):
-            for pair in range(2 * g, 2 * g + 2):
-                flipped[pair] = psum.tile([P, 2, 2, P], F32, name="flipped", tag="bank")
-                for a in range(2):
-                    words = w_raw[:, 2 * pair + a, :].bitcast(F32)
+            for half in range(2):
+                flipped[(g, half)] = psum.tile([P, 2, 2, P], F32, name="flipped", tag="bank")
+                for t in range(2):
+                    words = w_raw[:, g, 2 * half + t, :].bitcast(F32)
                     for u in range(2):
                         nc.tensor.transpose(
-                            flipped[pair][:, a, u, :], words[:, u :: 2], identity[:]
+                            flipped[(g, half)][:, t, u, :], words[:, u::2], identity[:]
                         )
 
         def regroup_w(g):
-            for pair in range(2 * g, 2 * g + 2):
-                dst = w_words[:, 2 * P * pair : 2 * P * (pair + 1), :].rearrange(
-                    "q (a o) u -> q a o u", a=2
+            for half in range(2):
+                nc.scalar.copy(
+                    out=w_words[:, g, :, 2 * half : 2 * half + 2, :],
+                    in_=flipped[(g, half)][:].rearrange("q t u m -> q m t u"),
                 )
-                src = flipped[pair][:].rearrange("q a u o -> q a o u")
-                if g % 2 == 0:
-                    nc.scalar.copy(out=dst, in_=src)
-                else:
-                    nc.vector.tensor_copy(out=dst, in_=src)
 
         def quantise_w(g):
             cols = slice(OUT_COLS * g, OUT_COLS * (g + 1))
@@ -149,120 +148,179 @@ def tile_multiheadselfattention_pa_t_kernel(tc, x, W_qkv, out_0, out_1, out_2):
                 in_=w_grouped[:, PACK * OUT_COLS * g : PACK * OUT_COLS * (g + 1)],
             )
 
-        pe = [const.tile([P, PACK, HALF_COLS], F32, name="pe%d" % s) for s in range(2)]
+        pe = [const.tile([P, PACK, ROWS, STEP], F32, name="pe%d" % c) for c in range(STEPS)]
 
-        def make_table(s, j):
-            angle = angles.tile([P, HALF_COLS], F32)
+        angles = {}
+        turns = {}
+
+        def table_angle(c, on_scalar):
+            begin = phase[:] if c == 0 else start[:, c - 1, :]
+            angles[c] = angle_pool.tile([P, PACK, STEP_COLS], F32, name="angle")
+            for j in range(PACK):
+                if on_scalar:
+                    nc.scalar.activation(
+                        out=angles[c][:, j, :], in_=position[:].rearrange("q m t -> q (m t)"),
+                        func=ACT.Identity, scale=rate[:, j : j + 1], bias=begin[:, j : j + 1],
+                    )
+                else:
+                    nc.vector.tensor_scalar(
+                        out=angles[c][:, j, :], in0=position[:].rearrange("q m t -> q (m t)"),
+                        scalar1=rate[:, j : j + 1], scalar2=begin[:, j : j + 1],
+                        op0=ALU.mult, op1=ALU.add,
+                    )
+
+        def table_round(c):
+            turns[c] = turn_pool.tile([P, PACK, STEP_COLS], F32, name="turn")
             nc.vector.tensor_scalar(
-                out=angle[:], in0=position[:, s, :, :].rearrange("q m t -> q (m t)"),
-                scalar1=rate[:, j : j + 1], scalar2=phase[:, j : j + 1], op0=ALU.mult, op1=ALU.add,
+                out=turns[c][:], in0=angles[c][:], scalar1=ROUND_MAGIC, scalar2=None, op0=ALU.add
             )
-            whole = angles.tile([P, HALF_COLS], F32)
-            nc.vector.tensor_scalar(
-                out=whole[:], in0=angle[:], scalar1=ROUND_MAGIC, scalar2=None, op0=ALU.add
-            )
-            back = angles.tile([P, HALF_COLS], F32)
+
+        def table_reduce(c):
             nc.vector.scalar_tensor_tensor(
-                out=back[:], in0=whole[:], scalar=ROUND_MAGIC, in1=angle[:],
+                out=turns[c][:], in0=turns[c][:], scalar=ROUND_MAGIC, in1=angles[c][:],
                 op0=ALU.subtract, op1=ALU.subtract,
             )
-            nc.scalar.activation(out=pe[s][:, j, :], in_=back[:], func=ACT.Sin, scale=-2.0 * math.pi)
 
-        token_tiles = {}
+        def table_sine(c):
+            nc.scalar.activation(
+                out=pe[c][:].rearrange("q j m t -> q (j m t)"),
+                in_=turns[c][:].rearrange("q j n -> q (j n)"), func=ACT.Sin, scale=-2.0 * math.pi,
+            )
 
-        def add_table(b, s):
-            if s == 0:
-                token_tiles[b] = (
-                    tokens.tile([P, RUN, GROUPS, PACK], BF16, name="grouped", align_bytes=64),
-                    tokens.tile([P, RUN, GROUPS], U32, name="codes", align_bytes=64),
-                    tokens.tile([P, RUN, GROUPS], U8, name="scales", align_bytes=64),
+        codes = {}
+        scales = {}
+        grouped = {}
+
+        def add_table(i, c, b):
+            if c == 0 and b == 0:
+                codes[i] = tokens.tile([P, RUN, P], U32, name="codes", align_bytes=64)
+                scales[i] = tokens.tile([P, RUN, P], U8, name="scales", align_bytes=64)
+            if b == 0:
+                grouped[(i, c)] = grouping.tile(
+                    [P, STEP, ROWS, PAIR, PACK], BF16, name="grouped", align_bytes=64
                 )
-            grouped = token_tiles[b][0]
-            half = slice(HALF_RUN * s, HALF_RUN * (s + 1))
             nc.vector.tensor_tensor(
-                out=grouped[:, half, :, :].rearrange("q t m j -> q m j t"),
-                in0=x_raw[b][:].rearrange("q j (m s t) -> q s m j t", s=2, t=HALF_RUN)[:, s],
-                in1=pe[s][:].rearrange("q j (m t) -> q m j t", t=HALF_RUN),
+                out=grouped[(i, c)][:, :, :, b, :].rearrange("q t m j -> q m j t"),
+                in0=x_raw[i][:, b, :, :].rearrange("q j (m c t) -> q c m j t", c=STEPS, t=STEP)[:, c],
+                in1=pe[c][:].rearrange("q j m t -> q m j t"),
                 op=ALU.add,
             )
 
-        def quantise_tokens(b, s):
-            grouped, codes, scales = token_tiles[b]
-            half = slice(HALF_RUN * s, HALF_RUN * (s + 1))
+        def quantise_tokens(i, c):
+            span = slice(STEP * c, STEP * (c + 1))
             nc.vector.quantize_mx(
-                out=codes[:, half, :].rearrange("q t m -> q (t m)").bitcast(FP8X4),
-                scales=scales[:, half, :].rearrange("q t m -> q (t m)"),
-                in_=grouped[:, half, :, :].rearrange("q t m j -> q (t m j)"),
+                out=codes[i][:, span, :].rearrange("q t m -> q (t m)").bitcast(FP8X4),
+                scales=scales[i][:, span, :].rearrange("q t m -> q (t m)"),
+                in_=grouped[(i, c)][:].rearrange("q t m b j -> q (t m b j)"),
             )
 
-        def prepare_tokens(b, step):
-            if step < 2:
-                add_table(b, step)
-            if step > 0:
-                quantise_tokens(b, step - 1)
+        stage = {}
 
-        stage_tiles = {}
-
-        def project(b, g, s):
-            codes, scales = token_tiles[b][1], token_tiles[b][2]
+        def project(i, g, t, engine_is_vector):
+            if (i, g) not in stage:
+                stage[(i, g)] = staging.tile([P, HEADS, RUN, HEAD_DIM], F32, name="stage")
             cols = slice(OUT_COLS * g, OUT_COLS * (g + 1))
-            if s == 0:
-                stage_tiles[(b, g)] = staging.tile([P, HEADS, RUN, HEAD_DIM], F32, name="stage")
-            stage = stage_tiles[(b, g)]
-            for t in range(HALF_RUN * s, HALF_RUN * (s + 1)):
-                acc = psum.tile([P, OUT_COLS], F32, tag="bank")
-                nc.tensor.matmul_mx(
-                    out=acc[:],
-                    lhsT=codes[:, t, :].bitcast(FP8X4),
-                    lhsT_scale=scales[:, t, :],
-                    rhs=w_codes[:, cols].bitcast(FP8X4),
-                    rhs_scale=w_scales[:, cols],
-                    start=True,
-                    stop=True,
-                )
-                by_head = acc[:].rearrange("m (h d) -> m h d", d=HEAD_DIM)
-                if t % 4 == 3:
-                    nc.vector.tensor_copy(out=stage[:, :, t, :], in_=by_head)
-                else:
-                    nc.scalar.copy(out=stage[:, :, t, :], in_=by_head)
-
-        def store(b, g, part, parts):
-            nc.sync.dma_start(
-                out=outs[g][b].rearrange("h (m c r) d -> c m h (r d)", c=parts, r=RUN // parts)[part],
-                in_=stage_tiles[(b, g)][:].rearrange("m h (c r) d -> m c h (r d)", c=parts)[:, part],
+            acc = psum.tile([P, OUT_COLS], F32, tag="bank")
+            nc.tensor.matmul_mx(
+                out=acc[:],
+                lhsT=codes[i][:, t, :].bitcast(FP8X4),
+                lhsT_scale=scales[i][:, t, :],
+                rhs=w_codes[:, cols].bitcast(FP8X4),
+                rhs_scale=w_scales[:, cols],
+                start=True,
+                stop=True,
             )
+            by_head = acc[:].rearrange("m (h d) -> m h d", d=HEAD_DIM)
+            if engine_is_vector:
+                nc.vector.tensor_copy(out=stage[(i, g)][:, :, t, :], in_=by_head)
+            else:
+                nc.scalar.copy(out=stage[(i, g)][:, :, t, :], in_=by_head)
 
-        for j in range(PACK):
-            make_table(0, j)
+        def store(i, g, t0, t1):
+            span = slice(HEAD_DIM * t0, HEAD_DIM * t1)
+            for b in range(PAIR):
+                nc.sync.dma_start(
+                    out=outs[g][PAIR * i + b].rearrange("h (m t) d -> m h (t d)", t=RUN)[:, :, span],
+                    in_=stage[(i, g)][:].rearrange("p h t d -> p h (t d)")[b::PAIR, :, span],
+                )
+
+        def project_steps(i, g, c0, c1, on_vector=()):
+            for n, t in enumerate(range(STEP * c0, STEP * c1)):
+                project(i, g, t, n in on_vector)
+
+        make_start(1)
+        make_start(2)
+        table_angle(0, False)
+        table_angle(1, True)
+        table_round(0)
+        table_reduce(0)
+        table_angle(2, True)
         flip_w(0)
-        flip_w(1)
         regroup_w(0)
-        for j in range(PACK):
-            make_table(1, j)
-        flip_w(2)
-        add_table(0, 0)
+        table_sine(0)
+        table_round(1)
+        table_reduce(1)
+        table_sine(1)
+        make_start(3)
+        table_angle(3, True)
+        add_table(0, 0, 0)
+        add_table(0, 0, 1)
         quantise_w(0)
         quantise_tokens(0, 0)
+        flip_w(1)
         regroup_w(1)
-        quantise_w(1)
-        project(0, 0, 0)
-        store(0, 0, 0, 2)
+        add_table(0, 1, 0)
+        project_steps(0, 0, 0, 1, (3,))
+        store(0, 0, 0, STEP)
+        flip_w(2)
         regroup_w(2)
-        add_table(0, 1)
-        quantise_w(2)
+        quantise_w(1)
+        add_table(0, 1, 1)
+        project_steps(0, 1, 0, 1, (3,))
+        store(0, 1, 0, STEP)
         quantise_tokens(0, 1)
-        for g in range(1, 3):
-            project(0, g, 0)
-            store(0, g, 0, 2)
-        for g in range(3):
-            project(0, g, 1)
-            store(0, g, 1, 2)
-            prepare_tokens(1, g)
+        quantise_w(2)
+        project_steps(0, 0, 1, 2)
+        store(0, 0, STEP, 2 * STEP)
+        table_round(2)
+        table_reduce(2)
+        table_sine(2)
+        project_steps(0, 1, 1, 2)
+        store(0, 1, STEP, 2 * STEP)
+        table_round(3)
+        table_reduce(3)
+        add_table(0, 2, 0)
+        add_table(0, 2, 1)
+        project_steps(0, 2, 0, 2, (2, 4, 6))
+        store(0, 2, 0, 2 * STEP)
+        quantise_tokens(0, 2)
+        table_sine(3)
+        project_steps(0, 0, 2, 3)
+        add_table(0, 3, 0)
+        add_table(0, 3, 1)
+        quantise_tokens(0, 3)
+        project_steps(0, 0, 3, 4, (1, 3))
+        store(0, 0, 2 * STEP, RUN)
+        add_table(1, 0, 0)
+        add_table(1, 0, 1)
+        project_steps(0, 1, 2, 4)
+        store(0, 1, 2 * STEP, RUN)
+        quantise_tokens(1, 0)
+        add_table(1, 1, 0)
+        add_table(1, 1, 1)
+        project_steps(0, 2, 2, 4)
+        store(0, 2, 2 * STEP, RUN)
+        quantise_tokens(1, 1)
+        add_table(1, 2, 0)
+        add_table(1, 2, 1)
+        project_steps(1, 0, 0, 2)
+        quantise_tokens(1, 2)
+        add_table(1, 3, 0)
+        add_table(1, 3, 1)
+        quantise_tokens(1, 3)
+        project_steps(1, 0, 2, 4, (5, 7))
+        store(1, 0, 0, RUN)
 
-        for b in range(1, BATCH):
-            for g in range(3):
-                project(b, g, 0)
-                project(b, g, 1)
-                store(b, g, 0, 1)
-                if b + 1 < BATCH:
-                    prepare_tokens(b + 1, g)
+        for g in range(1, THIRDS):
+            project_steps(1, g, 0, STEPS, range(1, RUN, 2))
+            store(1, g, 0, RUN)

@@ -38,8 +38,8 @@ def tile_multiheadselfattention_pa_t_kernel(tc, x, W_qkv, out_0, out_1, out_2):
     outs = [out_0, out_1, out_2]
     with ExitStack() as ctx:
         const = ctx.enter_context(tc.tile_pool(name="const", bufs=1))
-        angle_pool = ctx.enter_context(tc.tile_pool(name="angle_pool", bufs=3))
-        turn_pool = ctx.enter_context(tc.tile_pool(name="turn_pool", bufs=2))
+        bend_pool = ctx.enter_context(tc.tile_pool(name="bend_pool", bufs=2))
+        w_pool = ctx.enter_context(tc.tile_pool(name="w_pool", bufs=2))
         tokens = ctx.enter_context(tc.tile_pool(name="tokens", bufs=2))
         grouping = ctx.enter_context(tc.tile_pool(name="grouping", bufs=3))
         staging = ctx.enter_context(tc.tile_pool(name="staging", bufs=3))
@@ -109,16 +109,7 @@ def tile_multiheadselfattention_pa_t_kernel(tc, x, W_qkv, out_0, out_1, out_2):
             out=rate[:], in0=power[:], scalar1=lift[:, 0:1], scalar2=1.0 / (2.0 * math.pi),
             op0=ALU.mult, op1=ALU.mult,
         )
-        start = const.tile([P, STEPS - 1, PACK], F32)
-
-        def make_start(c):
-            nc.vector.scalar_tensor_tensor(
-                out=start[:, c - 1, :], in0=rate[:], scalar=float(STEP * c), in1=phase[:],
-                op0=ALU.mult, op1=ALU.add,
-            )
-
-        w_grouped = const.tile([P, THIRDS * OUT_COLS * PACK], BF16, align_bytes=64)
-        w_words = w_grouped[:].bitcast(F32).rearrange("q (g m t u) -> q g m t u", g=THIRDS, t=4, u=2)
+        w_grouped = {}
         w_codes = const.tile([P, THIRDS * OUT_COLS], U32, align_bytes=64)
         w_scales = const.tile([P, THIRDS * OUT_COLS], U8, align_bytes=64)
         flipped = {}
@@ -134,9 +125,11 @@ def tile_multiheadselfattention_pa_t_kernel(tc, x, W_qkv, out_0, out_1, out_2):
                         )
 
         def regroup_w(g):
+            w_grouped[g] = w_pool.tile([P, OUT_COLS * PACK], BF16, name="w_grouped", align_bytes=64)
+            words = w_grouped[g][:].bitcast(F32).rearrange("q (m t u) -> q m t u", t=4, u=2)
             for half in range(2):
                 nc.scalar.copy(
-                    out=w_words[:, g, :, 2 * half : 2 * half + 2, :],
+                    out=words[:, :, 2 * half : 2 * half + 2, :],
                     in_=flipped[(g, half)][:].rearrange("q t u m -> q m t u"),
                 )
 
@@ -145,64 +138,99 @@ def tile_multiheadselfattention_pa_t_kernel(tc, x, W_qkv, out_0, out_1, out_2):
             nc.vector.quantize_mx(
                 out=w_codes[:, cols].bitcast(FP8X4),
                 scales=w_scales[:, cols],
-                in_=w_grouped[:, PACK * OUT_COLS * g : PACK * OUT_COLS * (g + 1)],
+                in_=w_grouped[g][:],
             )
 
-        pe = [const.tile([P, PACK, ROWS, STEP], F32, name="pe%d" % c) for c in range(STEPS)]
+        pe = [const.tile([P, ROWS, PACK, STEP], F32, name="pe%d" % c) for c in range(STEPS)]
 
-        angles = {}
-        turns = {}
+        angle = const.tile([P, PACK, STEP_COLS], F32)
+        back = const.tile([P, PACK, STEP_COLS], F32)
+        ahead = const.tile([P, STEPS - 1, PACK], F32)
+        ahead_whole = const.tile([P, STEPS - 1, PACK], F32)
+        lag = const.tile([P, STEPS - 1, PACK], F32)
+        half_side = const.tile([P, STEPS - 1, PACK], F32)
+        side = const.tile([P, STEPS - 1, PACK], F32)
+        shift = const.tile([P, STEPS - 1, PACK], F32)
+        slope = const.tile([P, STEPS - 1, PACK], F32)
+        offset = const.tile([P, STEPS - 1, PACK], F32)
 
-        def table_angle(c, on_scalar):
-            begin = phase[:] if c == 0 else start[:, c - 1, :]
-            angles[c] = angle_pool.tile([P, PACK, STEP_COLS], F32, name="angle")
+        def make_back():
             for j in range(PACK):
-                if on_scalar:
-                    nc.scalar.activation(
-                        out=angles[c][:, j, :], in_=position[:].rearrange("q m t -> q (m t)"),
-                        func=ACT.Identity, scale=rate[:, j : j + 1], bias=begin[:, j : j + 1],
-                    )
-                else:
-                    nc.vector.tensor_scalar(
-                        out=angles[c][:, j, :], in0=position[:].rearrange("q m t -> q (m t)"),
-                        scalar1=rate[:, j : j + 1], scalar2=begin[:, j : j + 1],
-                        op0=ALU.mult, op1=ALU.add,
-                    )
-
-        def table_round(c):
-            turns[c] = turn_pool.tile([P, PACK, STEP_COLS], F32, name="turn")
+                nc.vector.tensor_scalar(
+                    out=angle[:, j, :], in0=position[:].rearrange("q m t -> q (m t)"),
+                    scalar1=rate[:, j : j + 1], scalar2=phase[:, j : j + 1], op0=ALU.mult, op1=ALU.add,
+                )
+            for c in range(1, STEPS):
+                nc.vector.tensor_scalar(
+                    out=ahead[:, c - 1, :], in0=rate[:], scalar1=float(STEP * c), scalar2=None, op0=ALU.mult
+                )
+            whole = const.tile([P, PACK, STEP_COLS], F32)
             nc.vector.tensor_scalar(
-                out=turns[c][:], in0=angles[c][:], scalar1=ROUND_MAGIC, scalar2=None, op0=ALU.add
+                out=whole[:], in0=angle[:], scalar1=ROUND_MAGIC, scalar2=None, op0=ALU.add
             )
-
-        def table_reduce(c):
+            nc.vector.tensor_scalar(
+                out=ahead_whole[:], in0=ahead[:], scalar1=ROUND_MAGIC, scalar2=None, op0=ALU.add
+            )
             nc.vector.scalar_tensor_tensor(
-                out=turns[c][:], in0=turns[c][:], scalar=ROUND_MAGIC, in1=angles[c][:],
+                out=back[:], in0=whole[:], scalar=ROUND_MAGIC, in1=angle[:],
                 op0=ALU.subtract, op1=ALU.subtract,
             )
-
-        def table_sine(c):
-            nc.scalar.activation(
-                out=pe[c][:].rearrange("q j m t -> q (j m t)"),
-                in_=turns[c][:].rearrange("q j n -> q (j n)"), func=ACT.Sin, scale=-2.0 * math.pi,
+            nc.vector.scalar_tensor_tensor(
+                out=lag[:], in0=ahead_whole[:], scalar=ROUND_MAGIC, in1=ahead[:],
+                op0=ALU.subtract, op1=ALU.subtract,
             )
+            nc.vector.tensor_scalar(
+                out=half_side[:], in0=lag[:], scalar1=0.0, scalar2=0.5, op0=ALU.is_le, op1=ALU.mult
+            )
+            nc.vector.tensor_scalar(
+                out=side[:], in0=half_side[:], scalar1=-0.25, scalar2=None, op0=ALU.add
+            )
+            nc.vector.tensor_tensor(out=shift[:], in0=lag[:], in1=side[:], op=ALU.add)
+            nc.vector.tensor_scalar(
+                out=slope[:], in0=side[:], scalar1=-8.0 * math.pi, scalar2=None, op0=ALU.mult
+            )
+            nc.vector.tensor_scalar(
+                out=offset[:], in0=side[:], scalar1=2.0 * math.pi, scalar2=None, op0=ALU.mult
+            )
+
+        bends = {}
+
+        def make_bend(c):
+            bends[c] = bend_pool.tile([P, PACK, STEP_COLS], F32, name="bend")
+            for j in range(PACK):
+                nc.scalar.activation(
+                    out=bends[c][:, j, :], in_=back[:, j, :], func=ACT.Abs, bias=shift[:, c - 1, j : j + 1]
+                )
+
+        def make_table(c):
+            if c == 0:
+                nc.scalar.activation(
+                    out=pe[0][:].rearrange("q m j t -> q j m t"),
+                    in_=back[:].rearrange("q j (m t) -> q j m t", t=STEP), func=ACT.Sin,
+                    scale=-2.0 * math.pi,
+                )
+            else:
+                for j in range(PACK):
+                    nc.scalar.activation(
+                        out=pe[c][:, :, j, :], in_=bends[c][:, j, :].rearrange("q (m t) -> q m t", t=STEP),
+                        func=ACT.Sin, scale=slope[:, c - 1, j : j + 1], bias=offset[:, c - 1, j : j + 1],
+                    )
 
         codes = {}
         scales = {}
         grouped = {}
 
-        def add_table(i, c, b):
-            if c == 0 and b == 0:
+        def add_table(i, c):
+            if c == 0:
                 codes[i] = tokens.tile([P, RUN, P], U32, name="codes", align_bytes=64)
                 scales[i] = tokens.tile([P, RUN, P], U8, name="scales", align_bytes=64)
-            if b == 0:
-                grouped[(i, c)] = grouping.tile(
-                    [P, STEP, ROWS, PAIR, PACK], BF16, name="grouped", align_bytes=64
-                )
+            grouped[(i, c)] = grouping.tile(
+                [P, STEP, ROWS, PAIR, PACK], BF16, name="grouped", align_bytes=64
+            )
             nc.vector.tensor_tensor(
-                out=grouped[(i, c)][:, :, :, b, :].rearrange("q t m j -> q m j t"),
-                in0=x_raw[i][:, b, :, :].rearrange("q j (m c t) -> q c m j t", c=STEPS, t=STEP)[:, c],
-                in1=pe[c][:].rearrange("q j m t -> q m j t"),
+                out=grouped[(i, c)][:].rearrange("q t m b j -> q m b j t"),
+                in0=x_raw[i][:].rearrange("q b j (m c t) -> q c m b j t", c=STEPS, t=STEP)[:, c],
+                in1=pe[c][:].unsqueeze(2).to_broadcast([P, ROWS, PAIR, PACK, STEP]),
                 op=ALU.add,
             )
 
@@ -248,78 +276,61 @@ def tile_multiheadselfattention_pa_t_kernel(tc, x, W_qkv, out_0, out_1, out_2):
             for n, t in enumerate(range(STEP * c0, STEP * c1)):
                 project(i, g, t, n in on_vector)
 
-        make_start(1)
-        make_start(2)
-        table_angle(0, False)
-        table_angle(1, True)
-        table_round(0)
-        table_reduce(0)
-        table_angle(2, True)
+        make_back()
         flip_w(0)
         regroup_w(0)
-        table_sine(0)
-        table_round(1)
-        table_reduce(1)
-        table_sine(1)
-        make_start(3)
-        table_angle(3, True)
-        add_table(0, 0, 0)
-        add_table(0, 0, 1)
+        make_table(0)
         quantise_w(0)
-        quantise_tokens(0, 0)
+        add_table(0, 0)
+        make_bend(1)
+        make_table(1)
+        make_bend(2)
         flip_w(1)
         regroup_w(1)
-        add_table(0, 1, 0)
-        project_steps(0, 0, 0, 1, (3,))
+        quantise_tokens(0, 0)
+        quantise_w(1)
+        project_steps(0, 0, 0, 1, (1, 3))
         store(0, 0, 0, STEP)
+        add_table(0, 1)
+        make_table(2)
+        project_steps(0, 1, 0, 1)
+        store(0, 1, 0, STEP)
         flip_w(2)
         regroup_w(2)
-        quantise_w(1)
-        add_table(0, 1, 1)
-        project_steps(0, 1, 0, 1, (3,))
-        store(0, 1, 0, STEP)
         quantise_tokens(0, 1)
-        quantise_w(2)
-        project_steps(0, 0, 1, 2)
+        project_steps(0, 0, 1, 2, (1, 3))
         store(0, 0, STEP, 2 * STEP)
-        table_round(2)
-        table_reduce(2)
-        table_sine(2)
-        project_steps(0, 1, 1, 2)
-        store(0, 1, STEP, 2 * STEP)
-        table_round(3)
-        table_reduce(3)
-        add_table(0, 2, 0)
-        add_table(0, 2, 1)
-        project_steps(0, 2, 0, 2, (2, 4, 6))
+        quantise_w(2)
+        project_steps(0, 2, 0, 2, (1, 7))
+        add_table(0, 2)
         store(0, 2, 0, 2 * STEP)
         quantise_tokens(0, 2)
-        table_sine(3)
+        project_steps(0, 1, 1, 2, (1, 3))
+        make_bend(3)
+        make_table(3)
+        project_steps(0, 1, 2, 3, (1, 3))
+        store(0, 1, STEP, 3 * STEP)
+        add_table(0, 3)
         project_steps(0, 0, 2, 3)
-        add_table(0, 3, 0)
-        add_table(0, 3, 1)
         quantise_tokens(0, 3)
         project_steps(0, 0, 3, 4, (1, 3))
         store(0, 0, 2 * STEP, RUN)
-        add_table(1, 0, 0)
-        add_table(1, 0, 1)
-        project_steps(0, 1, 2, 4)
-        store(0, 1, 2 * STEP, RUN)
-        quantise_tokens(1, 0)
-        add_table(1, 1, 0)
-        add_table(1, 1, 1)
+        add_table(1, 0)
         project_steps(0, 2, 2, 4)
         store(0, 2, 2 * STEP, RUN)
+        quantise_tokens(1, 0)
+        add_table(1, 1)
+        project_steps(0, 1, 3, 4)
+        store(0, 1, 3 * STEP, RUN)
         quantise_tokens(1, 1)
-        add_table(1, 2, 0)
-        add_table(1, 2, 1)
         project_steps(1, 0, 0, 2)
+        store(1, 0, 0, 2 * STEP)
+        add_table(1, 2)
         quantise_tokens(1, 2)
-        add_table(1, 3, 0)
-        add_table(1, 3, 1)
+        add_table(1, 3)
         quantise_tokens(1, 3)
-        project_steps(1, 0, 2, 4, (5, 7))
-        store(1, 0, 0, RUN)
+        project_steps(1, 0, 2, 4, (1, 3, 5, 7))
+        store(1, 0, 2 * STEP, RUN)
 
         for g in range(1, THIRDS):
             project_steps(1, g, 0, STEPS, range(1, RUN, 2))

@@ -74,41 +74,43 @@ def tile_multiheadselfattention_pa_t_kernel(tc, x, W_qkv, out_0, out_1, out_2):
         warm = const.tile([P, 1], F32)
         nc.scalar.activation(out=warm[:], in_=zero[:], func=ACT.Sin)
 
-        channel = const.tile([P, PACK], F32)
+        channel = const.tile([P, 1], F32)
         nc.gpsimd.iota(
-            channel[:], pattern=[[1, PACK]], base=0, channel_multiplier=PACK,
+            channel[:], pattern=[[1, 1]], base=0, channel_multiplier=PACK,
             allow_small_or_imprecise_dtypes=True,
         )
-        depth = const.tile([P, PACK], F32)
+        depth = const.tile([P, 1], F32)
         nc.gpsimd.tensor_scalar(
             out=depth[:], in0=channel[:], scalar1=-1.0 / 256.0, scalar2=0.0, op0=ALU.mult, op1=ALU.add
         )
-        ten_thousand = const.tile([P, PACK], F32)
+        ten_thousand = const.tile([P, 1], F32)
         nc.vector.memset(ten_thousand[:], 10000.0)
+        power = const.tile([P, 1], F32)
+        nc.gpsimd.tensor_tensor(out=power[:], in0=ten_thousand[:], in1=depth[:], op=ALU.pow)
         position = const.tile([P, ROWS, STEP], F32)
         nc.gpsimd.iota(
             position[:], pattern=[[RUN, ROWS], [1, STEP]], base=0, channel_multiplier=0,
             allow_small_or_imprecise_dtypes=True,
         )
-        power = const.tile([P, PACK], F32)
-        nc.gpsimd.tensor_tensor(out=power[:], in0=ten_thousand[:], in1=depth[:], op=ALU.pow)
         identity = const.tile([P, P], F32)
         make_identity(nc, identity[:])
-        phase = const.tile([P, PACK], F32)
+        phase = const.tile([P, 1], F32)
         nc.vector.tensor_scalar(
             out=phase[:], in0=channel[:], scalar1=256.0, scalar2=0.25, op0=ALU.is_ge, op1=ALU.mult
         )
-        beyond = const.tile([P, PACK], F32)
+        beyond = const.tile([P, 1], F32)
         nc.vector.tensor_scalar(
             out=beyond[:], in0=channel[:], scalar1=256.0, scalar2=9999.0, op0=ALU.is_ge, op1=ALU.mult
         )
-        lift = const.tile([P, PACK], F32)
+        lift = const.tile([P, 1], F32)
         nc.vector.tensor_scalar(out=lift[:], in0=beyond[:], scalar1=1.0, scalar2=None, op0=ALU.add)
         rate = const.tile([P, PACK], F32)
-        nc.vector.tensor_scalar(
-            out=rate[:], in0=power[:], scalar1=lift[:, 0:1], scalar2=1.0 / (2.0 * math.pi),
-            op0=ALU.mult, op1=ALU.mult,
-        )
+        for j in range(PACK):
+            nc.vector.tensor_scalar(
+                out=rate[:, j : j + 1], in0=power[:], scalar1=lift[:],
+                scalar2=10000.0 ** (-j / 256.0) / (2.0 * math.pi), op0=ALU.mult, op1=ALU.mult,
+            )
+
         w_grouped = {}
         w_codes = const.tile([P, THIRDS * OUT_COLS], U32, align_bytes=64)
         w_scales = const.tile([P, THIRDS * OUT_COLS], U8, align_bytes=64)
@@ -124,14 +126,20 @@ def tile_multiheadselfattention_pa_t_kernel(tc, x, W_qkv, out_0, out_1, out_2):
                             flipped[(g, half)][:, t, u, :], words[:, u::2], identity[:]
                         )
 
-        def regroup_w(g):
-            w_grouped[g] = w_pool.tile([P, OUT_COLS * PACK], BF16, name="w_grouped", align_bytes=64)
+        def regroup_half(g, half, on_vector=False):
+            if half == 0:
+                w_grouped[g] = w_pool.tile([P, OUT_COLS * PACK], BF16, name="w_grouped", align_bytes=64)
             words = w_grouped[g][:].bitcast(F32).rearrange("q (m t u) -> q m t u", t=4, u=2)
-            for half in range(2):
-                nc.scalar.copy(
-                    out=words[:, :, 2 * half : 2 * half + 2, :],
-                    in_=flipped[(g, half)][:].rearrange("q t u m -> q m t u"),
-                )
+            dst = words[:, :, 2 * half : 2 * half + 2, :]
+            src = flipped[(g, half)][:].rearrange("q t u m -> q m t u")
+            if on_vector:
+                nc.vector.tensor_copy(out=dst, in_=src)
+            else:
+                nc.scalar.copy(out=dst, in_=src)
+
+        def regroup_w(g):
+            regroup_half(g, 0)
+            regroup_half(g, 1)
 
         def quantise_w(g):
             cols = slice(OUT_COLS * g, OUT_COLS * (g + 1))
@@ -154,37 +162,49 @@ def tile_multiheadselfattention_pa_t_kernel(tc, x, W_qkv, out_0, out_1, out_2):
         slope = const.tile([P, STEPS - 1, PACK], F32)
         offset = const.tile([P, STEPS - 1, PACK], F32)
 
-        def make_back():
+        whole = const.tile([P, PACK, STEP_COLS], F32)
+
+        def make_back(w_copies):
+            halves = (slice(0, 2), slice(2, 4))
             for j in range(PACK):
                 nc.vector.tensor_scalar(
                     out=angle[:, j, :], in0=position[:].rearrange("q m t -> q (m t)"),
-                    scalar1=rate[:, j : j + 1], scalar2=phase[:, j : j + 1], op0=ALU.mult, op1=ALU.add,
+                    scalar1=rate[:, j : j + 1], scalar2=phase[:], op0=ALU.mult, op1=ALU.add,
                 )
             for c in range(1, STEPS):
                 nc.vector.tensor_scalar(
                     out=ahead[:, c - 1, :], in0=rate[:], scalar1=float(STEP * c), scalar2=None, op0=ALU.mult
                 )
-            whole = const.tile([P, PACK, STEP_COLS], F32)
-            nc.vector.tensor_scalar(
-                out=whole[:], in0=angle[:], scalar1=ROUND_MAGIC, scalar2=None, op0=ALU.add
-            )
+
+            def round_angle(h):
+                nc.vector.tensor_scalar(
+                    out=whole[:, h, :], in0=angle[:, h, :], scalar1=ROUND_MAGIC, scalar2=None, op0=ALU.add
+                )
+
+            def reduce_angle(h):
+                nc.vector.scalar_tensor_tensor(
+                    out=back[:, h, :], in0=whole[:, h, :], scalar=ROUND_MAGIC, in1=angle[:, h, :],
+                    op0=ALU.subtract, op1=ALU.subtract,
+                )
+
+            round_angle(halves[0])
             nc.vector.tensor_scalar(
                 out=ahead_whole[:], in0=ahead[:], scalar1=ROUND_MAGIC, scalar2=None, op0=ALU.add
             )
-            nc.vector.scalar_tensor_tensor(
-                out=back[:], in0=whole[:], scalar=ROUND_MAGIC, in1=angle[:],
-                op0=ALU.subtract, op1=ALU.subtract,
-            )
+            round_angle(halves[1])
             nc.vector.scalar_tensor_tensor(
                 out=lag[:], in0=ahead_whole[:], scalar=ROUND_MAGIC, in1=ahead[:],
                 op0=ALU.subtract, op1=ALU.subtract,
             )
+            reduce_angle(halves[0])
             nc.vector.tensor_scalar(
                 out=half_side[:], in0=lag[:], scalar1=0.0, scalar2=0.5, op0=ALU.is_le, op1=ALU.mult
             )
+            reduce_angle(halves[1])
             nc.vector.tensor_scalar(
                 out=side[:], in0=half_side[:], scalar1=-0.25, scalar2=None, op0=ALU.add
             )
+            w_copies[0]()
             nc.vector.tensor_tensor(out=shift[:], in0=lag[:], in1=side[:], op=ALU.add)
             nc.vector.tensor_scalar(
                 out=slope[:], in0=side[:], scalar1=-8.0 * math.pi, scalar2=None, op0=ALU.mult
@@ -192,6 +212,7 @@ def tile_multiheadselfattention_pa_t_kernel(tc, x, W_qkv, out_0, out_1, out_2):
             nc.vector.tensor_scalar(
                 out=offset[:], in0=side[:], scalar1=2.0 * math.pi, scalar2=None, op0=ALU.mult
             )
+            w_copies[1]()
 
         bends = {}
 
@@ -204,11 +225,12 @@ def tile_multiheadselfattention_pa_t_kernel(tc, x, W_qkv, out_0, out_1, out_2):
 
         def make_table(c):
             if c == 0:
-                nc.scalar.activation(
-                    out=pe[0][:].rearrange("q m j t -> q j m t"),
-                    in_=back[:].rearrange("q j (m t) -> q j m t", t=STEP), func=ACT.Sin,
-                    scale=-2.0 * math.pi,
-                )
+                for h in (slice(0, 2), slice(2, 4)):
+                    nc.scalar.activation(
+                        out=pe[0][:, :, h, :].rearrange("q m j t -> q j m t"),
+                        in_=back[:, h, :].rearrange("q j (m t) -> q j m t", t=STEP), func=ACT.Sin,
+                        scale=-2.0 * math.pi,
+                    )
             else:
                 for j in range(PACK):
                     nc.scalar.activation(
@@ -276,44 +298,50 @@ def tile_multiheadselfattention_pa_t_kernel(tc, x, W_qkv, out_0, out_1, out_2):
             for n, t in enumerate(range(STEP * c0, STEP * c1)):
                 project(i, g, t, n in on_vector)
 
-        make_back()
+        def keep_warm(n):
+            for k in range(n):
+                idle = psum.tile([P, CHANNELS], F32, name="idle", tag="bank")
+                nc.tensor.matmul(
+                    idle[:], w_raw[:, 0, 0, 0:P], w_raw[:, 0, 0, :], start=True, stop=True
+                )
+
         flip_w(0)
-        regroup_w(0)
+        make_back((lambda: regroup_half(0, 0, True), lambda: regroup_half(0, 1, True)))
         make_table(0)
         quantise_w(0)
-        add_table(0, 0)
         make_bend(1)
         make_table(1)
+        add_table(0, 0)
         make_bend(2)
         flip_w(1)
         regroup_w(1)
+        make_table(2)
         quantise_tokens(0, 0)
         quantise_w(1)
+        keep_warm(4)
         project_steps(0, 0, 0, 1, (1, 3))
         store(0, 0, 0, STEP)
         add_table(0, 1)
-        make_table(2)
         project_steps(0, 1, 0, 1)
         store(0, 1, 0, STEP)
         flip_w(2)
         regroup_w(2)
-        quantise_tokens(0, 1)
-        project_steps(0, 0, 1, 2, (1, 3))
-        store(0, 0, STEP, 2 * STEP)
-        quantise_w(2)
-        project_steps(0, 2, 0, 2, (1, 7))
-        add_table(0, 2)
-        store(0, 2, 0, 2 * STEP)
-        quantise_tokens(0, 2)
-        project_steps(0, 1, 1, 2, (1, 3))
         make_bend(3)
+        quantise_tokens(0, 1)
+        quantise_w(2)
+        keep_warm(4)
+        add_table(0, 2)
+        project_steps(0, 0, 1, 2)
+        store(0, 0, STEP, 2 * STEP)
         make_table(3)
-        project_steps(0, 1, 2, 3, (1, 3))
-        store(0, 1, STEP, 3 * STEP)
+        quantise_tokens(0, 2)
+        project_steps(0, 2, 0, 2, (1, 3, 5, 7))
+        store(0, 2, 0, 2 * STEP)
         add_table(0, 3)
-        project_steps(0, 0, 2, 3)
+        project_steps(0, 1, 1, 3, (7,))
+        store(0, 1, STEP, 3 * STEP)
         quantise_tokens(0, 3)
-        project_steps(0, 0, 3, 4, (1, 3))
+        project_steps(0, 0, 2, 4, (1, 3, 5, 7))
         store(0, 0, 2 * STEP, RUN)
         add_table(1, 0)
         project_steps(0, 2, 2, 4)

@@ -28,6 +28,7 @@ RUN = POSITIONS // ROWS
 STEP = 4
 STEPS = RUN // STEP
 STEP_COLS = ROWS * STEP
+STAGING = 104 * 1024
 ROUND_MAGIC = 12582912.0
 
 FLOPS = 2 * BATCH * POSITIONS * CHANNELS * THIRDS * OUT_COLS
@@ -42,7 +43,7 @@ def tile_multiheadselfattention_pa_t_kernel(tc, x, W_qkv, out_0, out_1, out_2):
         w_pool = ctx.enter_context(tc.tile_pool(name="w_pool", bufs=2))
         tokens = ctx.enter_context(tc.tile_pool(name="tokens", bufs=2))
         grouping = ctx.enter_context(tc.tile_pool(name="grouping", bufs=3))
-        staging = ctx.enter_context(tc.tile_pool(name="staging", bufs=3))
+        staging = ctx.enter_context(tc.tile_pool(name="staging", bufs=1))
         psum = ctx.enter_context(tc.psum_pool(name="psum", bufs=8))
         ctx.enter_context(tc.manual_schedule())
 
@@ -256,19 +257,39 @@ def tile_multiheadselfattention_pa_t_kernel(tc, x, W_qkv, out_0, out_1, out_2):
                 op=ALU.add,
             )
 
-        def quantise_tokens(i, c):
-            span = slice(STEP * c, STEP * (c + 1))
-            nc.vector.quantize_mx(
-                out=codes[i][:, span, :].rearrange("q t m -> q (t m)").bitcast(FP8X4),
-                scales=scales[i][:, span, :].rearrange("q t m -> q (t m)"),
-                in_=grouped[(i, c)][:].rearrange("q t m b j -> q (t m b j)"),
-            )
+        def quantise_tokens(i, c, parts=1):
+            count = STEP // parts
+            for part in range(parts):
+                span = slice(STEP * c + count * part, STEP * c + count * (part + 1))
+                nc.vector.quantize_mx(
+                    out=codes[i][:, span, :].rearrange("q t m -> q (t m)").bitcast(FP8X4),
+                    scales=scales[i][:, span, :].rearrange("q t m -> q (t m)"),
+                    in_=grouped[(i, c)][:, count * part : count * (part + 1), :, :, :].rearrange(
+                        "q t m b j -> q (t m b j)"
+                    ),
+                )
 
+        pieces = [
+            (0, 0, 0, 1), (0, 1, 0, 1), (0, 0, 1, 2), (0, 2, 0, 2), (0, 1, 1, 3), (0, 0, 2, 4),
+            (0, 2, 2, 4), (0, 1, 3, 4), (1, 0, 0, 4), (1, 1, 0, 4), (1, 2, 0, 4),
+        ]
+        staged = {}
+        place = 0
+        for i, g, c0, c1 in pieces:
+            size = HEADS * STEP * (c1 - c0) * HEAD_DIM * 4
+            if place + size > STAGING:
+                place = 0
+            for c in range(c0, c1):
+                staged[(i, g, c)] = (place, c0, c1)
+            place += size
         stage = {}
 
         def project(i, g, t, engine_is_vector):
-            if (i, g) not in stage:
-                stage[(i, g)] = staging.tile([P, HEADS, RUN, HEAD_DIM], F32, name="stage")
+            offset, c0, c1 = staged[(i, g, t // STEP)]
+            if (i, g, c0) not in stage:
+                stage[(i, g, c0)] = staging.tile(
+                    [P, HEADS, STEP * (c1 - c0), HEAD_DIM], F32, name="stage%d%d%d" % (i, g, c0), offset=offset
+                )
             cols = slice(OUT_COLS * g, OUT_COLS * (g + 1))
             acc = psum.tile([P, OUT_COLS], F32, tag="bank")
             nc.tensor.matmul_mx(
@@ -281,17 +302,18 @@ def tile_multiheadselfattention_pa_t_kernel(tc, x, W_qkv, out_0, out_1, out_2):
                 stop=True,
             )
             by_head = acc[:].rearrange("m (h d) -> m h d", d=HEAD_DIM)
+            dst = stage[(i, g, c0)][:, :, t - STEP * c0, :]
             if engine_is_vector:
-                nc.vector.tensor_copy(out=stage[(i, g)][:, :, t, :], in_=by_head)
+                nc.vector.tensor_copy(out=dst, in_=by_head)
             else:
-                nc.scalar.copy(out=stage[(i, g)][:, :, t, :], in_=by_head)
+                nc.scalar.copy(out=dst, in_=by_head)
 
-        def store(i, g, t0, t1):
-            span = slice(HEAD_DIM * t0, HEAD_DIM * t1)
+        def store(i, g, c0, c1):
+            span = slice(HEAD_DIM * STEP * c0, HEAD_DIM * STEP * c1)
             for b in range(PAIR):
                 nc.sync.dma_start(
                     out=outs[g][PAIR * i + b].rearrange("h (m t) d -> m h (t d)", t=RUN)[:, :, span],
-                    in_=stage[(i, g)][:].rearrange("p h t d -> p h (t d)")[b::PAIR, :, span],
+                    in_=stage[(i, g, c0)][:].rearrange("p h t d -> p h (t d)")[b::PAIR],
                 )
 
         def project_steps(i, g, c0, c1, on_vector=()):
@@ -316,14 +338,14 @@ def tile_multiheadselfattention_pa_t_kernel(tc, x, W_qkv, out_0, out_1, out_2):
         flip_w(1)
         regroup_w(1)
         make_table(2)
-        quantise_tokens(0, 0)
+        quantise_tokens(0, 0, 2)
         quantise_w(1)
-        keep_warm(4)
+        keep_warm(2)
         project_steps(0, 0, 0, 1, (1, 3))
-        store(0, 0, 0, STEP)
+        store(0, 0, 0, 1)
         add_table(0, 1)
         project_steps(0, 1, 0, 1)
-        store(0, 1, 0, STEP)
+        store(0, 1, 0, 1)
         flip_w(2)
         regroup_w(2)
         make_bend(3)
@@ -332,34 +354,33 @@ def tile_multiheadselfattention_pa_t_kernel(tc, x, W_qkv, out_0, out_1, out_2):
         keep_warm(4)
         add_table(0, 2)
         project_steps(0, 0, 1, 2)
-        store(0, 0, STEP, 2 * STEP)
+        store(0, 0, 1, 2)
         make_table(3)
         quantise_tokens(0, 2)
         project_steps(0, 2, 0, 2, (1, 3, 5, 7))
-        store(0, 2, 0, 2 * STEP)
+        store(0, 2, 0, 2)
         add_table(0, 3)
         project_steps(0, 1, 1, 3, (7,))
-        store(0, 1, STEP, 3 * STEP)
+        store(0, 1, 1, 3)
         quantise_tokens(0, 3)
         project_steps(0, 0, 2, 4, (1, 3, 5, 7))
-        store(0, 0, 2 * STEP, RUN)
+        store(0, 0, 2, 4)
         add_table(1, 0)
         project_steps(0, 2, 2, 4)
-        store(0, 2, 2 * STEP, RUN)
+        store(0, 2, 2, 4)
         quantise_tokens(1, 0)
         add_table(1, 1)
         project_steps(0, 1, 3, 4)
-        store(0, 1, 3 * STEP, RUN)
+        store(0, 1, 3, 4)
         quantise_tokens(1, 1)
         project_steps(1, 0, 0, 2)
-        store(1, 0, 0, 2 * STEP)
         add_table(1, 2)
         quantise_tokens(1, 2)
         add_table(1, 3)
         quantise_tokens(1, 3)
         project_steps(1, 0, 2, 4, (1, 3, 5, 7))
-        store(1, 0, 2 * STEP, RUN)
+        store(1, 0, 0, 4)
 
         for g in range(1, THIRDS):
             project_steps(1, g, 0, STEPS, range(1, RUN, 2))
-            store(1, g, 0, RUN)
+            store(1, g, 0, 4)

@@ -270,8 +270,7 @@ def tile_multiheadselfattention_pa_t_kernel(tc, x, W_qkv, out_0, out_1, out_2):
                 )
 
         pieces = [
-            (0, 0, 0, 1), (0, 1, 0, 1), (0, 0, 1, 2), (0, 2, 0, 2), (0, 1, 1, 3), (0, 0, 2, 4),
-            (0, 2, 2, 4), (0, 1, 3, 4), (1, 0, 0, 4), (1, 1, 0, 4), (1, 2, 0, 4),
+            (0, 0, 0, 1), (0, 1, 0, 1), (0, 0, 1, 2), (0, 2, 0, 2), (0, 1, 1, 3), (0, 0, 2, 4), (0, 2, 2, 4), (0, 1, 3, 4), (1, 0, 0, 4), (1, 1, 0, 4), (1, 2, 0, 4),
         ]
         staged = {}
         place = 0
@@ -284,12 +283,17 @@ def tile_multiheadselfattention_pa_t_kernel(tc, x, W_qkv, out_0, out_1, out_2):
             place += size
         stage = {}
 
-        def project(i, g, t, engine_is_vector):
+        def stage_of(i, g, t):
             offset, c0, c1 = staged[(i, g, t // STEP)]
             if (i, g, c0) not in stage:
                 stage[(i, g, c0)] = staging.tile(
                     [P, HEADS, STEP * (c1 - c0), HEAD_DIM], F32, name="stage%d%d%d" % (i, g, c0), offset=offset
                 )
+            return stage[(i, g, c0)]
+
+        def project(i, g, t, engine_is_vector):
+            c0 = staged[(i, g, t // STEP)][1]
+            dst = stage_of(i, g, t)[:, :, t - STEP * c0, :]
             cols = slice(OUT_COLS * g, OUT_COLS * (g + 1))
             acc = psum.tile([P, OUT_COLS], F32, tag="bank")
             nc.tensor.matmul_mx(
@@ -302,30 +306,61 @@ def tile_multiheadselfattention_pa_t_kernel(tc, x, W_qkv, out_0, out_1, out_2):
                 stop=True,
             )
             by_head = acc[:].rearrange("m (h d) -> m h d", d=HEAD_DIM)
-            dst = stage[(i, g, c0)][:, :, t - STEP * c0, :]
             if engine_is_vector:
                 nc.vector.tensor_copy(out=dst, in_=by_head)
             else:
                 nc.scalar.copy(out=dst, in_=by_head)
 
-        def store(i, g, c0, c1):
+        def project_half(i, g, t, half, engine_is_vector):
+            dst = stage_of(i, g, t)
+            c0 = staged[(i, g, t // STEP)][1]
+            heads = slice(HEADS // 2 * half, HEADS // 2 * (half + 1))
+            first = OUT_COLS * g + OUT_COLS // 2 * half
+            cols = slice(first, first + OUT_COLS // 2)
+            acc = psum.tile([P, 2, OUT_COLS // 2], F32, tag="bank")
+            for n in range(2):
+                nc.tensor.matmul_mx(
+                    out=acc[:, n, :],
+                    lhsT=codes[i][:, t + n, :].bitcast(FP8X4),
+                    lhsT_scale=scales[i][:, t + n, :],
+                    rhs=w_codes[:, cols].bitcast(FP8X4),
+                    rhs_scale=w_scales[:, cols],
+                    start=True,
+                    stop=True,
+                )
+            by_head = acc[:].rearrange("m n (h d) -> m n h d", d=HEAD_DIM)
+            dst = dst[:, heads, t - STEP * c0 : t - STEP * c0 + 2, :].rearrange("m h n d -> m n h d")
+            if engine_is_vector:
+                nc.vector.tensor_copy(out=dst, in_=by_head)
+            else:
+                nc.scalar.copy(out=dst, in_=by_head)
+
+        def store(i, g, c0, c1, heads=slice(0, HEADS)):
             span = slice(HEAD_DIM * STEP * c0, HEAD_DIM * STEP * c1)
             for b in range(PAIR):
                 nc.sync.dma_start(
-                    out=outs[g][PAIR * i + b].rearrange("h (m t) d -> m h (t d)", t=RUN)[:, :, span],
-                    in_=stage[(i, g, c0)][:].rearrange("p h t d -> p h (t d)")[b::PAIR],
+                    out=outs[g][PAIR * i + b].rearrange("h (m t) d -> m h (t d)", t=RUN)[:, heads, span],
+                    in_=stage[(i, g, c0)][:].rearrange("p h t d -> p h (t d)")[b::PAIR, heads, :],
                 )
+
+        def store_half(i, g, c0, c1, half):
+            store(i, g, c0, c1, slice(HEADS // 2 * half, HEADS // 2 * (half + 1)))
+
+        def project_halves(i, g, c0, c1, half, on_vector=()):
+            for n, t in enumerate(range(STEP * c0, STEP * c1, 2)):
+                project_half(i, g, t, half, n in on_vector)
 
         def project_steps(i, g, c0, c1, on_vector=()):
             for n, t in enumerate(range(STEP * c0, STEP * c1)):
                 project(i, g, t, n in on_vector)
 
-        def keep_warm(n):
-            for k in range(n):
-                idle = psum.tile([P, CHANNELS], F32, name="idle", tag="bank")
-                nc.tensor.matmul(
-                    idle[:], w_raw[:, 0, 0, 0:P], w_raw[:, 0, 0, :], start=True, stop=True
-                )
+        def keep_warm(rows):
+            for k in range(2):
+                idle = psum.tile([P, OUT_COLS], F32, name="idle", tag="bank")
+                nc.tensor.matmul(idle[:], rows[:, 0:P], rows[:, 0:OUT_COLS], start=True, stop=True)
+
+        def sums(i, c):
+            return grouped[(i, c)][:].rearrange("q t m b j -> q (t m b j)")
 
         flip_w(0)
         make_back((lambda: regroup_half(0, 0, True), lambda: regroup_half(0, 1, True)))
@@ -340,9 +375,11 @@ def tile_multiheadselfattention_pa_t_kernel(tc, x, W_qkv, out_0, out_1, out_2):
         make_table(2)
         quantise_tokens(0, 0, 2)
         quantise_w(1)
-        keep_warm(2)
-        project_steps(0, 0, 0, 1, (1, 3))
-        store(0, 0, 0, 1)
+        keep_warm(w_raw[:, 1, 0, :])
+        project_halves(0, 0, 0, 1, 0, (1,))
+        store_half(0, 0, 0, 1, 0)
+        project_halves(0, 0, 0, 1, 1, (1,))
+        store_half(0, 0, 0, 1, 1)
         add_table(0, 1)
         project_steps(0, 1, 0, 1)
         store(0, 1, 0, 1)
@@ -351,17 +388,22 @@ def tile_multiheadselfattention_pa_t_kernel(tc, x, W_qkv, out_0, out_1, out_2):
         make_bend(3)
         quantise_tokens(0, 1)
         quantise_w(2)
-        keep_warm(4)
         add_table(0, 2)
-        project_steps(0, 0, 1, 2)
-        store(0, 0, 1, 2)
-        make_table(3)
+        project_halves(0, 0, 1, 2, 0)
+        store_half(0, 0, 1, 2, 0)
+        project_halves(0, 0, 1, 2, 1)
+        store_half(0, 0, 1, 2, 1)
         quantise_tokens(0, 2)
-        project_steps(0, 2, 0, 2, (1, 3, 5, 7))
-        store(0, 2, 0, 2)
+        project_halves(0, 2, 0, 2, 0, (3,))
+        store_half(0, 2, 0, 2, 0)
+        make_table(3)
+        project_halves(0, 2, 0, 2, 1, (0, 1, 2))
+        store_half(0, 2, 0, 2, 1)
         add_table(0, 3)
-        project_steps(0, 1, 1, 3, (7,))
-        store(0, 1, 1, 3)
+        project_halves(0, 1, 1, 3, 0)
+        store_half(0, 1, 1, 3, 0)
+        project_halves(0, 1, 1, 3, 1, (3,))
+        store_half(0, 1, 1, 3, 1)
         quantise_tokens(0, 3)
         project_steps(0, 0, 2, 4, (1, 3, 5, 7))
         store(0, 0, 2, 4)
@@ -373,14 +415,20 @@ def tile_multiheadselfattention_pa_t_kernel(tc, x, W_qkv, out_0, out_1, out_2):
         project_steps(0, 1, 3, 4)
         store(0, 1, 3, 4)
         quantise_tokens(1, 1)
-        project_steps(1, 0, 0, 2)
         add_table(1, 2)
+        project_halves(1, 0, 0, 2, 0)
+        project_halves(1, 0, 0, 2, 1)
         quantise_tokens(1, 2)
         add_table(1, 3)
-        quantise_tokens(1, 3)
-        project_steps(1, 0, 2, 4, (1, 3, 5, 7))
-        store(1, 0, 0, 4)
+        project_halves(1, 0, 2, 3, 0)
+        project_halves(1, 0, 2, 3, 1)
+        quantise_tokens(1, 3, 2)
+        keep_warm(sums(1, 3))
+        project_halves(1, 0, 3, 4, 0, (1,))
+        store_half(1, 0, 0, 4, 0)
+        project_halves(1, 0, 3, 4, 1, (1,))
+        store_half(1, 0, 0, 4, 1)
 
         for g in range(1, THIRDS):
             project_steps(1, g, 0, STEPS, range(1, RUN, 2))
-            store(1, g, 0, 4)
+            store(1, g, 0, STEPS)

@@ -28,6 +28,7 @@ RUN = POSITIONS // ROWS
 STEP = 4
 STEPS = RUN // STEP
 STEP_COLS = ROWS * STEP
+FOLDED = STEPS - 2
 STAGING = 104 * 1024
 ROUND_MAGIC = 12582912.0
 
@@ -86,13 +87,13 @@ def tile_multiheadselfattention_pa_t_kernel(tc, x, W_qkv, out_0, out_1, out_2):
         )
         ten_thousand = const.tile([P, 1], F32)
         nc.vector.memset(ten_thousand[:], 10000.0)
-        power = const.tile([P, 1], F32)
-        nc.gpsimd.tensor_tensor(out=power[:], in0=ten_thousand[:], in1=depth[:], op=ALU.pow)
-        position = const.tile([P, ROWS, STEP], F32)
+        count = const.tile([P, ROWS], F32)
         nc.gpsimd.iota(
-            position[:], pattern=[[RUN, ROWS], [1, STEP]], base=0, channel_multiplier=0,
+            count[:], pattern=[[1, ROWS]], base=0, channel_multiplier=0,
             allow_small_or_imprecise_dtypes=True,
         )
+        power = const.tile([P, 1], F32)
+        nc.gpsimd.tensor_tensor(out=power[:], in0=ten_thousand[:], in1=depth[:], op=ALU.pow)
         identity = const.tile([P, P], F32)
         make_identity(nc, identity[:])
         phase = const.tile([P, 1], F32)
@@ -105,6 +106,15 @@ def tile_multiheadselfattention_pa_t_kernel(tc, x, W_qkv, out_0, out_1, out_2):
         )
         lift = const.tile([P, 1], F32)
         nc.vector.tensor_scalar(out=lift[:], in0=beyond[:], scalar1=1.0, scalar2=None, op0=ALU.add)
+        position = const.tile([P, ROWS, STEP], F32)
+        nc.vector.scalar_tensor_tensor(
+            out=position[:], in0=count[:].unsqueeze(2).to_broadcast([P, ROWS, STEP]), scalar=float(RUN),
+            in1=count[:, 0:STEP].unsqueeze(1).to_broadcast([P, ROWS, STEP]), op0=ALU.mult, op1=ALU.add,
+        )
+        half_pi = const.tile([P, 1], F32)
+        nc.vector.tensor_scalar(
+            out=half_pi[:], in0=zero[:], scalar1=math.pi / 2, scalar2=None, op0=ALU.add
+        )
         rate = const.tile([P, PACK], F32)
         for j in range(PACK):
             nc.vector.tensor_scalar(
@@ -154,14 +164,14 @@ def tile_multiheadselfattention_pa_t_kernel(tc, x, W_qkv, out_0, out_1, out_2):
 
         angle = const.tile([P, PACK, STEP_COLS], F32)
         back = const.tile([P, PACK, STEP_COLS], F32)
-        ahead = const.tile([P, STEPS - 1, PACK], F32)
-        ahead_whole = const.tile([P, STEPS - 1, PACK], F32)
-        lag = const.tile([P, STEPS - 1, PACK], F32)
-        half_side = const.tile([P, STEPS - 1, PACK], F32)
-        side = const.tile([P, STEPS - 1, PACK], F32)
-        shift = const.tile([P, STEPS - 1, PACK], F32)
-        slope = const.tile([P, STEPS - 1, PACK], F32)
-        offset = const.tile([P, STEPS - 1, PACK], F32)
+        ahead = const.tile([P, FOLDED, PACK], F32)
+        ahead_whole = const.tile([P, FOLDED, PACK], F32)
+        lag = const.tile([P, FOLDED, PACK], F32)
+        half_side = const.tile([P, FOLDED, PACK], F32)
+        side = const.tile([P, FOLDED, PACK], F32)
+        shift = const.tile([P, FOLDED, PACK], F32)
+        slope = const.tile([P, FOLDED, PACK], F32)
+        offset = const.tile([P, FOLDED, PACK], F32)
 
         whole = const.tile([P, PACK, STEP_COLS], F32)
 
@@ -172,7 +182,7 @@ def tile_multiheadselfattention_pa_t_kernel(tc, x, W_qkv, out_0, out_1, out_2):
                     out=angle[:, j, :], in0=position[:].rearrange("q m t -> q (m t)"),
                     scalar1=rate[:, j : j + 1], scalar2=phase[:], op0=ALU.mult, op1=ALU.add,
                 )
-            for c in range(1, STEPS):
+            for c in range(1, FOLDED + 1):
                 nc.vector.tensor_scalar(
                     out=ahead[:, c - 1, :], in0=rate[:], scalar1=float(STEP * c), scalar2=None, op0=ALU.mult
                 )
@@ -214,6 +224,26 @@ def tile_multiheadselfattention_pa_t_kernel(tc, x, W_qkv, out_0, out_1, out_2):
                 out=offset[:], in0=side[:], scalar1=2.0 * math.pi, scalar2=None, op0=ALU.mult
             )
             w_copies[1]()
+
+        lag_size = const.tile([P, PACK], F32)
+        cosine = const.tile([P, PACK], F32)
+        twice = const.tile([P, PACK], F32)
+
+        def make_twice():
+            nc.scalar.activation(out=lag_size[:], in_=lag[:, 0, :], func=ACT.Abs)
+            nc.scalar.activation(
+                out=cosine[:], in_=lag_size[:], func=ACT.Sin, scale=-2.0 * math.pi, bias=half_pi[:]
+            )
+            nc.vector.tensor_scalar(
+                out=twice[:], in0=cosine[:], scalar1=2.0, scalar2=None, op0=ALU.mult
+            )
+
+        def make_last_table():
+            for j in range(PACK):
+                nc.vector.scalar_tensor_tensor(
+                    out=pe[STEPS - 1][:, :, j, :], in0=pe[STEPS - 2][:, :, j, :], scalar=twice[:, j : j + 1],
+                    in1=pe[STEPS - 3][:, :, j, :], op0=ALU.mult, op1=ALU.subtract,
+                )
 
         bends = {}
 
@@ -270,7 +300,7 @@ def tile_multiheadselfattention_pa_t_kernel(tc, x, W_qkv, out_0, out_1, out_2):
                 )
 
         pieces = [
-            (0, 0, 0, 1), (0, 1, 0, 1), (0, 0, 1, 2), (0, 2, 0, 2), (0, 1, 1, 3), (0, 0, 2, 4), (0, 2, 2, 4), (0, 1, 3, 4), (1, 0, 0, 4), (1, 1, 0, 4), (1, 2, 0, 4),
+            (0, 0, 0, 1), (0, 1, 0, 1), (0, 0, 1, 2), (0, 2, 0, 2), (0, 1, 1, 4), (0, 0, 2, 4), (0, 2, 2, 4), (1, 0, 0, 4), (1, 1, 0, 4), (1, 2, 0, 4),
         ]
         staged = {}
         place = 0
@@ -367,6 +397,7 @@ def tile_multiheadselfattention_pa_t_kernel(tc, x, W_qkv, out_0, out_1, out_2):
         make_table(0)
         quantise_w(0)
         make_bend(1)
+        make_twice()
         make_table(1)
         add_table(0, 0)
         make_bend(2)
@@ -381,11 +412,12 @@ def tile_multiheadselfattention_pa_t_kernel(tc, x, W_qkv, out_0, out_1, out_2):
         project_halves(0, 0, 0, 1, 1, (1,))
         store_half(0, 0, 0, 1, 1)
         add_table(0, 1)
-        project_steps(0, 1, 0, 1)
-        store(0, 1, 0, 1)
+        project_halves(0, 1, 0, 1, 0)
+        store_half(0, 1, 0, 1, 0)
+        project_halves(0, 1, 0, 1, 1)
+        store_half(0, 1, 0, 1, 1)
         flip_w(2)
         regroup_w(2)
-        make_bend(3)
         quantise_tokens(0, 1)
         quantise_w(2)
         add_table(0, 2)
@@ -393,27 +425,27 @@ def tile_multiheadselfattention_pa_t_kernel(tc, x, W_qkv, out_0, out_1, out_2):
         store_half(0, 0, 1, 2, 0)
         project_halves(0, 0, 1, 2, 1)
         store_half(0, 0, 1, 2, 1)
+        make_last_table()
         quantise_tokens(0, 2)
-        project_halves(0, 2, 0, 2, 0, (3,))
-        store_half(0, 2, 0, 2, 0)
-        make_table(3)
-        project_halves(0, 2, 0, 2, 1, (0, 1, 2))
-        store_half(0, 2, 0, 2, 1)
         add_table(0, 3)
-        project_halves(0, 1, 1, 3, 0)
-        store_half(0, 1, 1, 3, 0)
-        project_halves(0, 1, 1, 3, 1, (3,))
-        store_half(0, 1, 1, 3, 1)
+        project_halves(0, 2, 0, 2, 0)
+        store_half(0, 2, 0, 2, 0)
+        project_halves(0, 2, 0, 2, 1)
+        store_half(0, 2, 0, 2, 1)
         quantise_tokens(0, 3)
-        project_steps(0, 0, 2, 4, (1, 3, 5, 7))
-        store(0, 0, 2, 4)
+        project_halves(0, 1, 1, 3, 0, (2, 3))
+        keep_warm(sums(0, 3))
+        project_halves(0, 1, 3, 4, 0, (1,))
+        store_half(0, 1, 1, 4, 0)
+        project_halves(0, 1, 1, 4, 1)
+        store_half(0, 1, 1, 4, 1)
         add_table(1, 0)
-        project_steps(0, 2, 2, 4)
-        store(0, 2, 2, 4)
+        project_steps(0, 0, 2, 4, (7,))
+        store(0, 0, 2, 4)
         quantise_tokens(1, 0)
         add_table(1, 1)
-        project_steps(0, 1, 3, 4)
-        store(0, 1, 3, 4)
+        project_steps(0, 2, 2, 4, (7,))
+        store(0, 2, 2, 4)
         quantise_tokens(1, 1)
         add_table(1, 2)
         project_halves(1, 0, 0, 2, 0)

@@ -28,7 +28,6 @@ RUN = POSITIONS // ROWS
 STEP = 4
 STEPS = RUN // STEP
 STEP_COLS = ROWS * STEP
-FOLDED = STEPS - 2
 STAGING = 104 * 1024
 ROUND_MAGIC = 12582912.0
 
@@ -40,7 +39,6 @@ def tile_multiheadselfattention_pa_t_kernel(tc, x, W_qkv, out_0, out_1, out_2):
     outs = [out_0, out_1, out_2]
     with ExitStack() as ctx:
         const = ctx.enter_context(tc.tile_pool(name="const", bufs=1))
-        bend_pool = ctx.enter_context(tc.tile_pool(name="bend_pool", bufs=2))
         w_pool = ctx.enter_context(tc.tile_pool(name="w_pool", bufs=2))
         tokens = ctx.enter_context(tc.tile_pool(name="tokens", bufs=2))
         grouping = ctx.enter_context(tc.tile_pool(name="grouping", bufs=3))
@@ -164,14 +162,14 @@ def tile_multiheadselfattention_pa_t_kernel(tc, x, W_qkv, out_0, out_1, out_2):
 
         angle = const.tile([P, PACK, STEP_COLS], F32)
         back = const.tile([P, PACK, STEP_COLS], F32)
-        ahead = const.tile([P, FOLDED, PACK], F32)
-        ahead_whole = const.tile([P, FOLDED, PACK], F32)
-        lag = const.tile([P, FOLDED, PACK], F32)
-        half_side = const.tile([P, FOLDED, PACK], F32)
-        side = const.tile([P, FOLDED, PACK], F32)
-        shift = const.tile([P, FOLDED, PACK], F32)
-        slope = const.tile([P, FOLDED, PACK], F32)
-        offset = const.tile([P, FOLDED, PACK], F32)
+        ahead = const.tile([P, PACK], F32)
+        ahead_whole = const.tile([P, PACK], F32)
+        lag = const.tile([P, PACK], F32)
+        half_side = const.tile([P, PACK], F32)
+        side = const.tile([P, PACK], F32)
+        shift = const.tile([P, PACK], F32)
+        slope = const.tile([P, PACK], F32)
+        offset = const.tile([P, PACK], F32)
 
         whole = const.tile([P, PACK, STEP_COLS], F32)
 
@@ -182,10 +180,9 @@ def tile_multiheadselfattention_pa_t_kernel(tc, x, W_qkv, out_0, out_1, out_2):
                     out=angle[:, j, :], in0=position[:].rearrange("q m t -> q (m t)"),
                     scalar1=rate[:, j : j + 1], scalar2=phase[:], op0=ALU.mult, op1=ALU.add,
                 )
-            for c in range(1, FOLDED + 1):
-                nc.vector.tensor_scalar(
-                    out=ahead[:, c - 1, :], in0=rate[:], scalar1=float(STEP * c), scalar2=None, op0=ALU.mult
-                )
+            nc.vector.tensor_scalar(
+                out=ahead[:], in0=rate[:], scalar1=float(STEP), scalar2=None, op0=ALU.mult
+            )
 
             def round_angle(h):
                 nc.vector.tensor_scalar(
@@ -230,7 +227,7 @@ def tile_multiheadselfattention_pa_t_kernel(tc, x, W_qkv, out_0, out_1, out_2):
         twice = const.tile([P, PACK], F32)
 
         def make_twice():
-            nc.scalar.activation(out=lag_size[:], in_=lag[:, 0, :], func=ACT.Abs)
+            nc.scalar.activation(out=lag_size[:], in_=lag[:], func=ACT.Abs)
             nc.scalar.activation(
                 out=cosine[:], in_=lag_size[:], func=ACT.Sin, scale=-2.0 * math.pi, bias=half_pi[:]
             )
@@ -238,36 +235,35 @@ def tile_multiheadselfattention_pa_t_kernel(tc, x, W_qkv, out_0, out_1, out_2):
                 out=twice[:], in0=cosine[:], scalar1=2.0, scalar2=None, op0=ALU.mult
             )
 
-        def make_last_table():
+        def make_next_table(c):
             for j in range(PACK):
                 nc.vector.scalar_tensor_tensor(
-                    out=pe[STEPS - 1][:, :, j, :], in0=pe[STEPS - 2][:, :, j, :], scalar=twice[:, j : j + 1],
-                    in1=pe[STEPS - 3][:, :, j, :], op0=ALU.mult, op1=ALU.subtract,
+                    out=pe[c][:, :, j, :], in0=pe[c - 1][:, :, j, :], scalar=twice[:, j : j + 1],
+                    in1=pe[c - 2][:, :, j, :], op0=ALU.mult, op1=ALU.subtract,
                 )
 
-        bends = {}
+        bend = const.tile([P, PACK, STEP_COLS], F32)
 
-        def make_bend(c):
-            bends[c] = bend_pool.tile([P, PACK, STEP_COLS], F32, name="bend")
+        def make_bend():
             for j in range(PACK):
                 nc.scalar.activation(
-                    out=bends[c][:, j, :], in_=back[:, j, :], func=ACT.Abs, bias=shift[:, c - 1, j : j + 1]
+                    out=bend[:, j, :], in_=back[:, j, :], func=ACT.Abs, bias=shift[:, j : j + 1]
                 )
 
-        def make_table(c):
-            if c == 0:
-                for h in (slice(0, 2), slice(2, 4)):
-                    nc.scalar.activation(
-                        out=pe[0][:, :, h, :].rearrange("q m j t -> q j m t"),
-                        in_=back[:, h, :].rearrange("q j (m t) -> q j m t", t=STEP), func=ACT.Sin,
-                        scale=-2.0 * math.pi,
-                    )
-            else:
-                for j in range(PACK):
-                    nc.scalar.activation(
-                        out=pe[c][:, :, j, :], in_=bends[c][:, j, :].rearrange("q (m t) -> q m t", t=STEP),
-                        func=ACT.Sin, scale=slope[:, c - 1, j : j + 1], bias=offset[:, c - 1, j : j + 1],
-                    )
+        def make_first_table():
+            for h in (slice(0, 2), slice(2, 4)):
+                nc.scalar.activation(
+                    out=pe[0][:, :, h, :].rearrange("q m j t -> q j m t"),
+                    in_=back[:, h, :].rearrange("q j (m t) -> q j m t", t=STEP), func=ACT.Sin,
+                    scale=-2.0 * math.pi,
+                )
+
+        def make_second_table():
+            for j in range(PACK):
+                nc.scalar.activation(
+                    out=pe[1][:, :, j, :], in_=bend[:, j, :].rearrange("q (m t) -> q m t", t=STEP),
+                    func=ACT.Sin, scale=slope[:, j : j + 1], bias=offset[:, j : j + 1],
+                )
 
         codes = {}
         scales = {}
@@ -394,38 +390,36 @@ def tile_multiheadselfattention_pa_t_kernel(tc, x, W_qkv, out_0, out_1, out_2):
 
         flip_w(0)
         make_back((lambda: regroup_half(0, 0, True), lambda: regroup_half(0, 1, True)))
-        make_table(0)
+        make_first_table()
         quantise_w(0)
-        make_bend(1)
+        make_bend()
         make_twice()
-        make_table(1)
+        make_second_table()
         add_table(0, 0)
-        make_bend(2)
         flip_w(1)
         regroup_w(1)
-        make_table(2)
+        flip_w(2)
+        regroup_w(2)
         quantise_tokens(0, 0, 2)
         quantise_w(1)
-        keep_warm(w_raw[:, 1, 0, :])
-        project_halves(0, 0, 0, 1, 0, (1,))
+        project_halves(0, 0, 0, 1, 0)
         store_half(0, 0, 0, 1, 0)
-        project_halves(0, 0, 0, 1, 1, (1,))
+        project_halves(0, 0, 0, 1, 1)
         store_half(0, 0, 0, 1, 1)
         add_table(0, 1)
         project_halves(0, 1, 0, 1, 0)
         store_half(0, 1, 0, 1, 0)
         project_halves(0, 1, 0, 1, 1)
         store_half(0, 1, 0, 1, 1)
-        flip_w(2)
-        regroup_w(2)
-        quantise_tokens(0, 1)
         quantise_w(2)
+        quantise_tokens(0, 1)
+        make_next_table(2)
         add_table(0, 2)
         project_halves(0, 0, 1, 2, 0)
         store_half(0, 0, 1, 2, 0)
         project_halves(0, 0, 1, 2, 1)
         store_half(0, 0, 1, 2, 1)
-        make_last_table()
+        make_next_table(3)
         quantise_tokens(0, 2)
         add_table(0, 3)
         project_halves(0, 2, 0, 2, 0)
@@ -433,7 +427,7 @@ def tile_multiheadselfattention_pa_t_kernel(tc, x, W_qkv, out_0, out_1, out_2):
         project_halves(0, 2, 0, 2, 1)
         store_half(0, 2, 0, 2, 1)
         quantise_tokens(0, 3)
-        project_halves(0, 1, 1, 3, 0, (2, 3))
+        project_halves(0, 1, 1, 3, 0)
         keep_warm(sums(0, 3))
         project_halves(0, 1, 3, 4, 0, (1,))
         store_half(0, 1, 1, 4, 0)

@@ -21,6 +21,9 @@ HEADS = 8
 HEAD_DIM = 64
 OUT_COLS = HEADS * HEAD_DIM
 THIRDS = 3
+SIXTHS = 2 * THIRDS
+SIXTH_HEADS = HEADS // 2
+SIXTH_COLS = OUT_COLS // 2
 PAIR = 2
 PAIRS = BATCH // PAIR
 ROWS = P // PAIR
@@ -296,89 +299,55 @@ def tile_multiheadselfattention_pa_t_kernel(tc, x, W_qkv, out_0, out_1, out_2):
                 )
 
         pieces = [
-            (0, 0, 0, 1), (0, 1, 0, 1), (0, 0, 1, 2), (0, 2, 0, 2), (0, 1, 1, 4), (0, 0, 2, 4), (0, 2, 2, 4), (1, 0, 0, 4), (1, 1, 0, 4), (1, 2, 0, 4),
+            (0, 0, 0, 1), (0, 1, 0, 1), (0, 2, 0, 1), (0, 3, 0, 2), (0, 4, 0, 2), (0, 5, 0, 2), (0, 0, 1, 3), (0, 1, 1, 4), (0, 2, 1, 4), (0, 0, 3, 4), (0, 3, 2, 4), (0, 4, 2, 4), (0, 5, 2, 4), (1, 0, 0, 4), (1, 1, 0, 4), (1, 2, 0, 4), (1, 3, 0, 4), (1, 4, 0, 4), (1, 5, 0, 4),
         ]
         staged = {}
         place = 0
-        for i, g, c0, c1 in pieces:
-            size = HEADS * STEP * (c1 - c0) * HEAD_DIM * 4
+        for i, s, c0, c1 in pieces:
+            size = SIXTH_HEADS * STEP * (c1 - c0) * HEAD_DIM * 4
             if place + size > STAGING:
                 place = 0
             for c in range(c0, c1):
-                staged[(i, g, c)] = (place, c0, c1)
+                staged[(i, s, c)] = (place, c0, c1)
             place += size
         stage = {}
 
-        def stage_of(i, g, t):
-            offset, c0, c1 = staged[(i, g, t // STEP)]
-            if (i, g, c0) not in stage:
-                stage[(i, g, c0)] = staging.tile(
-                    [P, HEADS, STEP * (c1 - c0), HEAD_DIM], F32, name="stage%d%d%d" % (i, g, c0), offset=offset
-                )
-            return stage[(i, g, c0)]
+        def project(i, s, first, end, on_vector=()):
+            cols = slice(SIXTH_COLS * s, SIXTH_COLS * (s + 1))
+            for n, t in enumerate(range(STEP * first, STEP * end, 2)):
+                offset, c0, c1 = staged[(i, s, t // STEP)]
+                if (i, s, c0) not in stage:
+                    stage[(i, s, c0)] = staging.tile(
+                        [P, SIXTH_HEADS, STEP * (c1 - c0), HEAD_DIM], F32,
+                        name="stage%d%d%d" % (i, s, c0), offset=offset,
+                    )
+                acc = psum.tile([P, 2, SIXTH_COLS], F32, tag="bank")
+                for r in range(2):
+                    nc.tensor.matmul_mx(
+                        out=acc[:, r, :],
+                        lhsT=codes[i][:, t + r, :].bitcast(FP8X4),
+                        lhsT_scale=scales[i][:, t + r, :],
+                        rhs=w_codes[:, cols].bitcast(FP8X4),
+                        rhs_scale=w_scales[:, cols],
+                        start=True,
+                        stop=True,
+                    )
+                src = acc[:].rearrange("m r (h d) -> m r h d", d=HEAD_DIM)
+                place_in = t - STEP * c0
+                dst = stage[(i, s, c0)][:, :, place_in : place_in + 2, :].rearrange("m h r d -> m r h d")
+                if n in on_vector:
+                    nc.vector.tensor_copy(out=dst, in_=src)
+                else:
+                    nc.scalar.copy(out=dst, in_=src)
 
-        def project(i, g, t, engine_is_vector):
-            c0 = staged[(i, g, t // STEP)][1]
-            dst = stage_of(i, g, t)[:, :, t - STEP * c0, :]
-            cols = slice(OUT_COLS * g, OUT_COLS * (g + 1))
-            acc = psum.tile([P, OUT_COLS], F32, tag="bank")
-            nc.tensor.matmul_mx(
-                out=acc[:],
-                lhsT=codes[i][:, t, :].bitcast(FP8X4),
-                lhsT_scale=scales[i][:, t, :],
-                rhs=w_codes[:, cols].bitcast(FP8X4),
-                rhs_scale=w_scales[:, cols],
-                start=True,
-                stop=True,
-            )
-            by_head = acc[:].rearrange("m (h d) -> m h d", d=HEAD_DIM)
-            if engine_is_vector:
-                nc.vector.tensor_copy(out=dst, in_=by_head)
-            else:
-                nc.scalar.copy(out=dst, in_=by_head)
-
-        def project_half(i, g, t, half, engine_is_vector):
-            dst = stage_of(i, g, t)
-            c0 = staged[(i, g, t // STEP)][1]
-            heads = slice(HEADS // 2 * half, HEADS // 2 * (half + 1))
-            first = OUT_COLS * g + OUT_COLS // 2 * half
-            cols = slice(first, first + OUT_COLS // 2)
-            acc = psum.tile([P, 2, OUT_COLS // 2], F32, tag="bank")
-            for n in range(2):
-                nc.tensor.matmul_mx(
-                    out=acc[:, n, :],
-                    lhsT=codes[i][:, t + n, :].bitcast(FP8X4),
-                    lhsT_scale=scales[i][:, t + n, :],
-                    rhs=w_codes[:, cols].bitcast(FP8X4),
-                    rhs_scale=w_scales[:, cols],
-                    start=True,
-                    stop=True,
-                )
-            by_head = acc[:].rearrange("m n (h d) -> m n h d", d=HEAD_DIM)
-            dst = dst[:, heads, t - STEP * c0 : t - STEP * c0 + 2, :].rearrange("m h n d -> m n h d")
-            if engine_is_vector:
-                nc.vector.tensor_copy(out=dst, in_=by_head)
-            else:
-                nc.scalar.copy(out=dst, in_=by_head)
-
-        def store(i, g, c0, c1, heads=slice(0, HEADS)):
+        def store(i, s, c0, c1):
+            heads = slice(SIXTH_HEADS * (s % 2), SIXTH_HEADS * (s % 2 + 1))
             span = slice(HEAD_DIM * STEP * c0, HEAD_DIM * STEP * c1)
             for b in range(PAIR):
                 nc.sync.dma_start(
-                    out=outs[g][PAIR * i + b].rearrange("h (m t) d -> m h (t d)", t=RUN)[:, heads, span],
-                    in_=stage[(i, g, c0)][:].rearrange("p h t d -> p h (t d)")[b::PAIR, heads, :],
+                    out=outs[s // 2][PAIR * i + b].rearrange("h (m t) d -> m h (t d)", t=RUN)[:, heads, span],
+                    in_=stage[(i, s, c0)][:].rearrange("p h t d -> p h (t d)")[b::PAIR],
                 )
-
-        def store_half(i, g, c0, c1, half):
-            store(i, g, c0, c1, slice(HEADS // 2 * half, HEADS // 2 * (half + 1)))
-
-        def project_halves(i, g, c0, c1, half, on_vector=()):
-            for n, t in enumerate(range(STEP * c0, STEP * c1, 2)):
-                project_half(i, g, t, half, n in on_vector)
-
-        def project_steps(i, g, c0, c1, on_vector=()):
-            for n, t in enumerate(range(STEP * c0, STEP * c1)):
-                project(i, g, t, n in on_vector)
 
         def keep_warm(rows):
             for k in range(2):
@@ -402,59 +371,53 @@ def tile_multiheadselfattention_pa_t_kernel(tc, x, W_qkv, out_0, out_1, out_2):
         regroup_w(2)
         quantise_tokens(0, 0, 2)
         quantise_w(1)
-        project_halves(0, 0, 0, 1, 0)
-        store_half(0, 0, 0, 1, 0)
-        project_halves(0, 0, 0, 1, 1)
-        store_half(0, 0, 0, 1, 1)
+        for s in range(2):
+            project(0, s, 0, 1)
+            store(0, s, 0, 1)
         add_table(0, 1)
-        project_halves(0, 1, 0, 1, 0)
-        store_half(0, 1, 0, 1, 0)
-        project_halves(0, 1, 0, 1, 1)
-        store_half(0, 1, 0, 1, 1)
+        project(0, 2, 0, 1)
+        store(0, 2, 0, 1)
+        project(0, 3, 0, 1)
         quantise_w(2)
         quantise_tokens(0, 1)
+        project(0, 3, 1, 2)
+        store(0, 3, 0, 2)
         make_next_table(2)
         add_table(0, 2)
-        project_halves(0, 0, 1, 2, 0)
-        store_half(0, 0, 1, 2, 0)
-        project_halves(0, 0, 1, 2, 1)
-        store_half(0, 0, 1, 2, 1)
+        for s in range(4, 6):
+            project(0, s, 0, 2)
+            store(0, s, 0, 2)
         make_next_table(3)
         quantise_tokens(0, 2)
         add_table(0, 3)
-        project_halves(0, 2, 0, 2, 0)
-        store_half(0, 2, 0, 2, 0)
-        project_halves(0, 2, 0, 2, 1)
-        store_half(0, 2, 0, 2, 1)
+        project(0, 0, 1, 3)
+        store(0, 0, 1, 3)
+        project(0, 1, 1, 3)
         quantise_tokens(0, 3)
-        project_halves(0, 1, 1, 3, 0)
-        keep_warm(sums(0, 3))
-        project_halves(0, 1, 3, 4, 0, (1,))
-        store_half(0, 1, 1, 4, 0)
-        project_halves(0, 1, 1, 4, 1)
-        store_half(0, 1, 1, 4, 1)
+        project(0, 1, 3, 4, (1,))
+        store(0, 1, 1, 4)
         add_table(1, 0)
-        project_steps(0, 0, 2, 4, (7,))
-        store(0, 0, 2, 4)
+        project(0, 2, 1, 4, (5,))
+        store(0, 2, 1, 4)
         quantise_tokens(1, 0)
         add_table(1, 1)
-        project_steps(0, 2, 2, 4, (7,))
-        store(0, 2, 2, 4)
+        project(0, 0, 3, 4, (1,))
+        store(0, 0, 3, 4)
         quantise_tokens(1, 1)
         add_table(1, 2)
-        project_halves(1, 0, 0, 2, 0)
-        project_halves(1, 0, 0, 2, 1)
+        project(0, 3, 2, 4)
+        store(0, 3, 2, 4)
         quantise_tokens(1, 2)
         add_table(1, 3)
-        project_halves(1, 0, 2, 3, 0)
-        project_halves(1, 0, 2, 3, 1)
+        for s in range(4, 6):
+            project(0, s, 2, 4)
+            store(0, s, 2, 4)
+        project(1, 0, 0, 3)
         quantise_tokens(1, 3, 2)
         keep_warm(sums(1, 3))
-        project_halves(1, 0, 3, 4, 0, (1,))
-        store_half(1, 0, 0, 4, 0)
-        project_halves(1, 0, 3, 4, 1, (1,))
-        store_half(1, 0, 0, 4, 1)
+        project(1, 0, 3, 4, (1,))
+        store(1, 0, 0, 4)
 
-        for g in range(1, THIRDS):
-            project_steps(1, g, 0, STEPS, range(1, RUN, 2))
-            store(1, g, 0, STEPS)
+        for s in range(1, SIXTHS):
+            project(1, s, 0, STEPS, range(1, RUN // 2, 2))
+            store(1, s, 0, STEPS)

@@ -58,19 +58,17 @@ def tile_multiheadselfattention_pa_t_kernel(tc, x, W_qkv, out_0, out_1, out_2):
                 in_=W_qkv[OUT_COLS * g : OUT_COLS * (g + 1), :].rearrange("(m t) k -> m t k", t=4),
             )
 
-        def load_x(b):
+        def load_x(i):
             nc.sync.dma_start(
-                out=x_raw[b // PAIR][:, b % PAIR, :, :],
-                in_=x[b].rearrange("c h w -> c (h w)").rearrange("(q j) n -> q j n", j=PACK),
+                out=x_raw[i][:].rearrange("q b j n -> q b (j n)"),
+                in_=x[PAIR * i : PAIR * (i + 1)].rearrange("b (q j) h w -> q b (j h w)", j=PACK),
             )
 
         load_w(0)
         load_x(0)
-        load_x(1)
         load_w(1)
         load_w(2)
-        load_x(2)
-        load_x(3)
+        load_x(1)
 
         zero = const.tile([P, 1], F32)
         nc.vector.memset(zero[:], 0.0)
@@ -299,27 +297,30 @@ def tile_multiheadselfattention_pa_t_kernel(tc, x, W_qkv, out_0, out_1, out_2):
                 )
 
         pieces = [
-            (0, 0, 0, 1), (0, 1, 0, 1), (0, 2, 0, 1), (0, 3, 0, 2), (0, 4, 0, 2), (0, 5, 0, 2), (0, 0, 1, 3), (0, 1, 1, 4), (0, 2, 1, 4), (0, 0, 3, 4), (0, 3, 2, 4), (0, 4, 2, 4), (0, 5, 2, 4), (1, 0, 0, 4), (1, 1, 0, 4), (1, 2, 0, 4), (1, 3, 0, 4), (1, 4, 0, 4), (1, 5, 0, 4),
+            (0, 0, 1, 0, 1), (0, 1, 1, 0, 1), (0, 2, 1, 0, 1), (0, 3, 1, 0, 1), (0, 4, 1, 0, 2), (0, 5, 1, 0, 2), (0, 0, 1, 1, 3), (0, 1, 1, 1, 4), (0, 2, 1, 1, 4), (0, 3, 1, 1, 4), (0, 0, 1, 3, 4), (0, 4, 2, 2, 4), (1, 0, 1, 0, 4), (1, 1, 1, 0, 4), (1, 2, 2, 0, 4), (1, 4, 2, 0, 4),
         ]
         staged = {}
         place = 0
-        for i, s, c0, c1 in pieces:
-            size = SIXTH_HEADS * STEP * (c1 - c0) * HEAD_DIM * 4
+        for piece in pieces:
+            i, s0, n, c0, c1 = piece
+            size = SIXTH_HEADS * n * STEP * (c1 - c0) * HEAD_DIM * 4
             if place + size > STAGING:
                 place = 0
-            for c in range(c0, c1):
-                staged[(i, s, c)] = (place, c0, c1)
+            for s in range(s0, s0 + n):
+                for c in range(c0, c1):
+                    staged[(i, s, c)] = (place, piece)
             place += size
         stage = {}
 
         def project(i, s, first, end, on_vector=()):
             cols = slice(SIXTH_COLS * s, SIXTH_COLS * (s + 1))
-            for n, t in enumerate(range(STEP * first, STEP * end, 2)):
-                offset, c0, c1 = staged[(i, s, t // STEP)]
-                if (i, s, c0) not in stage:
-                    stage[(i, s, c0)] = staging.tile(
-                        [P, SIXTH_HEADS, STEP * (c1 - c0), HEAD_DIM], F32,
-                        name="stage%d%d%d" % (i, s, c0), offset=offset,
+            for k, t in enumerate(range(STEP * first, STEP * end, 2)):
+                offset, piece = staged[(i, s, t // STEP)]
+                s0, n, c0, c1 = piece[1:]
+                if piece not in stage:
+                    stage[piece] = staging.tile(
+                        [P, SIXTH_HEADS * n, STEP * (c1 - c0), HEAD_DIM], F32,
+                        name="stage%d%d%d" % (i, s0, c0), offset=offset,
                     )
                 acc = psum.tile([P, 2, SIXTH_COLS], F32, tag="bank")
                 for r in range(2):
@@ -333,20 +334,23 @@ def tile_multiheadselfattention_pa_t_kernel(tc, x, W_qkv, out_0, out_1, out_2):
                         stop=True,
                     )
                 src = acc[:].rearrange("m r (h d) -> m r h d", d=HEAD_DIM)
-                place_in = t - STEP * c0
-                dst = stage[(i, s, c0)][:, :, place_in : place_in + 2, :].rearrange("m h r d -> m r h d")
-                if n in on_vector:
+                heads = slice(SIXTH_HEADS * (s - s0), SIXTH_HEADS * (s - s0 + 1))
+                slots = slice(t - STEP * c0, t - STEP * c0 + 2)
+                dst = stage[piece][:, heads, slots, :].rearrange("m h r d -> m r h d")
+                if k in on_vector:
                     nc.vector.tensor_copy(out=dst, in_=src)
                 else:
                     nc.scalar.copy(out=dst, in_=src)
 
-        def store(i, s, c0, c1):
-            heads = slice(SIXTH_HEADS * (s % 2), SIXTH_HEADS * (s % 2 + 1))
+        def store(i, s, c):
+            piece = staged[(i, s, c)][1]
+            s0, n, c0, c1 = piece[1:]
+            heads = slice(SIXTH_HEADS * (s0 % 2), SIXTH_HEADS * (s0 % 2 + n))
             span = slice(HEAD_DIM * STEP * c0, HEAD_DIM * STEP * c1)
             for b in range(PAIR):
                 nc.sync.dma_start(
-                    out=outs[s // 2][PAIR * i + b].rearrange("h (m t) d -> m h (t d)", t=RUN)[:, heads, span],
-                    in_=stage[(i, s, c0)][:].rearrange("p h t d -> p h (t d)")[b::PAIR],
+                    out=outs[s0 // 2][PAIR * i + b].rearrange("h (m t) d -> m h (t d)", t=RUN)[:, heads, span],
+                    in_=stage[piece][:].rearrange("p h t d -> p h (t d)")[b::PAIR],
                 )
 
         def keep_warm(rows):
@@ -373,51 +377,52 @@ def tile_multiheadselfattention_pa_t_kernel(tc, x, W_qkv, out_0, out_1, out_2):
         quantise_w(1)
         for s in range(2):
             project(0, s, 0, 1)
-            store(0, s, 0, 1)
+            store(0, s, 0)
         add_table(0, 1)
-        project(0, 2, 0, 1)
-        store(0, 2, 0, 1)
-        project(0, 3, 0, 1)
+        for s in range(2, 4):
+            project(0, s, 0, 1)
+            store(0, s, 0)
         quantise_w(2)
         quantise_tokens(0, 1)
-        project(0, 3, 1, 2)
-        store(0, 3, 0, 2)
         make_next_table(2)
         add_table(0, 2)
         for s in range(4, 6):
             project(0, s, 0, 2)
-            store(0, s, 0, 2)
+            store(0, s, 0)
         make_next_table(3)
         quantise_tokens(0, 2)
         add_table(0, 3)
         project(0, 0, 1, 3)
-        store(0, 0, 1, 3)
+        store(0, 0, 1)
         project(0, 1, 1, 3)
         quantise_tokens(0, 3)
         project(0, 1, 3, 4, (1,))
-        store(0, 1, 1, 4)
+        store(0, 1, 1)
         add_table(1, 0)
         project(0, 2, 1, 4, (5,))
-        store(0, 2, 1, 4)
+        store(0, 2, 1)
         quantise_tokens(1, 0)
         add_table(1, 1)
+        project(0, 3, 1, 4)
+        store(0, 3, 1)
         project(0, 0, 3, 4, (1,))
-        store(0, 0, 3, 4)
+        store(0, 0, 3)
         quantise_tokens(1, 1)
         add_table(1, 2)
-        project(0, 3, 2, 4)
-        store(0, 3, 2, 4)
         quantise_tokens(1, 2)
         add_table(1, 3)
         for s in range(4, 6):
             project(0, s, 2, 4)
-            store(0, s, 2, 4)
+        store(0, 4, 2)
         project(1, 0, 0, 3)
         quantise_tokens(1, 3, 2)
         keep_warm(sums(1, 3))
         project(1, 0, 3, 4, (1,))
-        store(1, 0, 0, 4)
+        store(1, 0, 0)
 
-        for s in range(1, SIXTHS):
+        project(1, 1, 0, STEPS, range(1, RUN // 2, 2))
+        store(1, 1, 0)
+        for s in range(2, SIXTHS, 2):
             project(1, s, 0, STEPS, range(1, RUN // 2, 2))
-            store(1, s, 0, STEPS)
+            project(1, s + 1, 0, STEPS, range(1, RUN // 2, 2))
+            store(1, s, 0)

import math
from contextlib import ExitStack

import concourse.mybir as mybir
from concourse.masks import make_identity

F32 = mybir.dt.float32
BF16 = mybir.dt.bfloat16
U32 = mybir.dt.uint32
U8 = mybir.dt.uint8
FP8X4 = mybir.dt.float8_e4m3fn_x4
ALU = mybir.AluOpType
ACT = mybir.ActivationFunctionType

P = 128
PACK = 4
BATCH = 4
CHANNELS = 512
POSITIONS = 1024
HEADS = 8
HEAD_DIM = 64
OUT_COLS = HEADS * HEAD_DIM
THIRDS = 3
SIXTHS = 2 * THIRDS
SIXTH_HEADS = HEADS // 2
SIXTH_COLS = OUT_COLS // 2
PAIR = 2
PAIRS = BATCH // PAIR
ROWS = P // PAIR
RUN = POSITIONS // ROWS
STEP = 4
STEPS = RUN // STEP
STEP_COLS = ROWS * STEP
STAGING = 104 * 1024
ROUND_MAGIC = 12582912.0

FLOPS = 2 * BATCH * POSITIONS * CHANNELS * THIRDS * OUT_COLS


def tile_multiheadselfattention_pa_t_kernel(tc, x, W_qkv, out_0, out_1, out_2):
    nc = tc.nc
    outs = [out_0, out_1, out_2]
    with ExitStack() as ctx:
        const = ctx.enter_context(tc.tile_pool(name="const", bufs=1))
        w_pool = ctx.enter_context(tc.tile_pool(name="w_pool", bufs=2))
        tokens = ctx.enter_context(tc.tile_pool(name="tokens", bufs=2))
        grouping = ctx.enter_context(tc.tile_pool(name="grouping", bufs=3))
        staging = ctx.enter_context(tc.tile_pool(name="staging", bufs=1))
        psum = ctx.enter_context(tc.psum_pool(name="psum", bufs=8))
        ctx.enter_context(tc.manual_schedule())

        w_raw = const.tile([P, THIRDS, 4, CHANNELS], BF16)
        x_raw = [const.tile([P, PAIR, PACK, POSITIONS], BF16, name="x_raw%d" % i) for i in range(PAIRS)]

        def load_w(g):
            nc.sync.dma_start(
                out=w_raw[:, g, :, :],
                in_=W_qkv[OUT_COLS * g : OUT_COLS * (g + 1), :].rearrange("(m t) k -> m t k", t=4),
            )

        def load_x(i):
            nc.sync.dma_start(
                out=x_raw[i][:].rearrange("q b j n -> q b (j n)"),
                in_=x[PAIR * i : PAIR * (i + 1)].rearrange("b (q j) h w -> q b (j h w)", j=PACK),
            )

        load_w(0)
        load_x(0)
        load_w(1)
        load_w(2)
        load_x(1)

        zero = const.tile([P, 1], F32)
        nc.vector.memset(zero[:], 0.0)
        warm = const.tile([P, 1], F32)
        nc.scalar.activation(out=warm[:], in_=zero[:], func=ACT.Sin)

        channel = const.tile([P, 1], F32)
        nc.gpsimd.iota(
            channel[:], pattern=[[1, 1]], base=0, channel_multiplier=PACK,
            allow_small_or_imprecise_dtypes=True,
        )
        depth = const.tile([P, 1], F32)
        nc.gpsimd.tensor_scalar(
            out=depth[:], in0=channel[:], scalar1=-1.0 / 256.0, scalar2=0.0, op0=ALU.mult, op1=ALU.add
        )
        ten_thousand = const.tile([P, 1], F32)
        nc.vector.memset(ten_thousand[:], 10000.0)
        count = const.tile([P, ROWS], F32)
        nc.gpsimd.iota(
            count[:], pattern=[[1, ROWS]], base=0, channel_multiplier=0,
            allow_small_or_imprecise_dtypes=True,
        )
        power = const.tile([P, 1], F32)
        nc.gpsimd.tensor_tensor(out=power[:], in0=ten_thousand[:], in1=depth[:], op=ALU.pow)
        identity = const.tile([P, P], F32)
        make_identity(nc, identity[:])
        phase = const.tile([P, 1], F32)
        nc.vector.tensor_scalar(
            out=phase[:], in0=channel[:], scalar1=256.0, scalar2=0.25, op0=ALU.is_ge, op1=ALU.mult
        )
        beyond = const.tile([P, 1], F32)
        nc.vector.tensor_scalar(
            out=beyond[:], in0=channel[:], scalar1=256.0, scalar2=9999.0, op0=ALU.is_ge, op1=ALU.mult
        )
        lift = const.tile([P, 1], F32)
        nc.vector.tensor_scalar(out=lift[:], in0=beyond[:], scalar1=1.0, scalar2=None, op0=ALU.add)
        position = const.tile([P, ROWS, STEP], F32)
        nc.vector.scalar_tensor_tensor(
            out=position[:], in0=count[:].unsqueeze(2).to_broadcast([P, ROWS, STEP]), scalar=float(RUN),
            in1=count[:, 0:STEP].unsqueeze(1).to_broadcast([P, ROWS, STEP]), op0=ALU.mult, op1=ALU.add,
        )
        half_pi = const.tile([P, 1], F32)
        nc.vector.tensor_scalar(
            out=half_pi[:], in0=zero[:], scalar1=math.pi / 2, scalar2=None, op0=ALU.add
        )
        rate = const.tile([P, PACK], F32)
        for j in range(PACK):
            nc.vector.tensor_scalar(
                out=rate[:, j : j + 1], in0=power[:], scalar1=lift[:],
                scalar2=10000.0 ** (-j / 256.0) / (2.0 * math.pi), op0=ALU.mult, op1=ALU.mult,
            )

        w_grouped = {}
        w_codes = const.tile([P, THIRDS * OUT_COLS], U32, align_bytes=64)
        w_scales = const.tile([P, THIRDS * OUT_COLS], U8, align_bytes=64)
        flipped = {}

        def flip_w(g):
            for half in range(2):
                flipped[(g, half)] = psum.tile([P, 2, 2, P], F32, name="flipped", tag="bank")
                for t in range(2):
                    words = w_raw[:, g, 2 * half + t, :].bitcast(F32)
                    for u in range(2):
                        nc.tensor.transpose(
                            flipped[(g, half)][:, t, u, :], words[:, u::2], identity[:]
                        )

        def regroup_half(g, half, on_vector=False):
            if half == 0:
                w_grouped[g] = w_pool.tile([P, OUT_COLS * PACK], BF16, name="w_grouped", align_bytes=64)
            words = w_grouped[g][:].bitcast(F32).rearrange("q (m t u) -> q m t u", t=4, u=2)
            dst = words[:, :, 2 * half : 2 * half + 2, :]
            src = flipped[(g, half)][:].rearrange("q t u m -> q m t u")
            if on_vector:
                nc.vector.tensor_copy(out=dst, in_=src)
            else:
                nc.scalar.copy(out=dst, in_=src)

        def regroup_w(g):
            regroup_half(g, 0)
            regroup_half(g, 1)

        def quantise_w(g):
            cols = slice(OUT_COLS * g, OUT_COLS * (g + 1))
            nc.vector.quantize_mx(
                out=w_codes[:, cols].bitcast(FP8X4),
                scales=w_scales[:, cols],
                in_=w_grouped[g][:],
            )

        pe = [const.tile([P, ROWS, PACK, STEP], F32, name="pe%d" % c) for c in range(STEPS)]

        angle = const.tile([P, PACK, STEP_COLS], F32)
        back = const.tile([P, PACK, STEP_COLS], F32)
        ahead = const.tile([P, PACK], F32)
        ahead_whole = const.tile([P, PACK], F32)
        lag = const.tile([P, PACK], F32)
        half_side = const.tile([P, PACK], F32)
        side = const.tile([P, PACK], F32)
        shift = const.tile([P, PACK], F32)
        slope = const.tile([P, PACK], F32)
        offset = const.tile([P, PACK], F32)

        whole = const.tile([P, PACK, STEP_COLS], F32)

        def make_back(w_copies):
            halves = (slice(0, 2), slice(2, 4))
            for j in range(PACK):
                nc.vector.tensor_scalar(
                    out=angle[:, j, :], in0=position[:].rearrange("q m t -> q (m t)"),
                    scalar1=rate[:, j : j + 1], scalar2=phase[:], op0=ALU.mult, op1=ALU.add,
                )
            nc.vector.tensor_scalar(
                out=ahead[:], in0=rate[:], scalar1=float(STEP), scalar2=None, op0=ALU.mult
            )

            def round_angle(h):
                nc.vector.tensor_scalar(
                    out=whole[:, h, :], in0=angle[:, h, :], scalar1=ROUND_MAGIC, scalar2=None, op0=ALU.add
                )

            def reduce_angle(h):
                nc.vector.scalar_tensor_tensor(
                    out=back[:, h, :], in0=whole[:, h, :], scalar=ROUND_MAGIC, in1=angle[:, h, :],
                    op0=ALU.subtract, op1=ALU.subtract,
                )

            round_angle(halves[0])
            nc.vector.tensor_scalar(
                out=ahead_whole[:], in0=ahead[:], scalar1=ROUND_MAGIC, scalar2=None, op0=ALU.add
            )
            round_angle(halves[1])
            nc.vector.scalar_tensor_tensor(
                out=lag[:], in0=ahead_whole[:], scalar=ROUND_MAGIC, in1=ahead[:],
                op0=ALU.subtract, op1=ALU.subtract,
            )
            reduce_angle(halves[0])
            nc.vector.tensor_scalar(
                out=half_side[:], in0=lag[:], scalar1=0.0, scalar2=0.5, op0=ALU.is_le, op1=ALU.mult
            )
            reduce_angle(halves[1])
            nc.vector.tensor_scalar(
                out=side[:], in0=half_side[:], scalar1=-0.25, scalar2=None, op0=ALU.add
            )
            w_copies[0]()
            nc.vector.tensor_tensor(out=shift[:], in0=lag[:], in1=side[:], op=ALU.add)
            nc.vector.tensor_scalar(
                out=slope[:], in0=side[:], scalar1=-8.0 * math.pi, scalar2=None, op0=ALU.mult
            )
            nc.vector.tensor_scalar(
                out=offset[:], in0=side[:], scalar1=2.0 * math.pi, scalar2=None, op0=ALU.mult
            )
            w_copies[1]()

        lag_size = const.tile([P, PACK], F32)
        cosine = const.tile([P, PACK], F32)
        twice = const.tile([P, PACK], F32)

        def make_twice():
            nc.scalar.activation(out=lag_size[:], in_=lag[:], func=ACT.Abs)
            nc.scalar.activation(
                out=cosine[:], in_=lag_size[:], func=ACT.Sin, scale=-2.0 * math.pi, bias=half_pi[:]
            )
            nc.vector.tensor_scalar(
                out=twice[:], in0=cosine[:], scalar1=2.0, scalar2=None, op0=ALU.mult
            )

        def make_next_table(c):
            for j in range(PACK):
                nc.vector.scalar_tensor_tensor(
                    out=pe[c][:, :, j, :], in0=pe[c - 1][:, :, j, :], scalar=twice[:, j : j + 1],
                    in1=pe[c - 2][:, :, j, :], op0=ALU.mult, op1=ALU.subtract,
                )

        bend = const.tile([P, PACK, STEP_COLS], F32)

        def make_bend():
            for j in range(PACK):
                nc.scalar.activation(
                    out=bend[:, j, :], in_=back[:, j, :], func=ACT.Abs, bias=shift[:, j : j + 1]
                )

        def make_first_table():
            for h in (slice(0, 2), slice(2, 4)):
                nc.scalar.activation(
                    out=pe[0][:, :, h, :].rearrange("q m j t -> q j m t"),
                    in_=back[:, h, :].rearrange("q j (m t) -> q j m t", t=STEP), func=ACT.Sin,
                    scale=-2.0 * math.pi,
                )

        def make_second_table():
            for j in range(PACK):
                nc.scalar.activation(
                    out=pe[1][:, :, j, :], in_=bend[:, j, :].rearrange("q (m t) -> q m t", t=STEP),
                    func=ACT.Sin, scale=slope[:, j : j + 1], bias=offset[:, j : j + 1],
                )

        codes = {}
        scales = {}
        grouped = {}

        def add_table(i, c):
            if c == 0:
                codes[i] = tokens.tile([P, RUN, P], U32, name="codes", align_bytes=64)
                scales[i] = tokens.tile([P, RUN, P], U8, name="scales", align_bytes=64)
            grouped[(i, c)] = grouping.tile(
                [P, STEP, ROWS, PAIR, PACK], BF16, name="grouped", align_bytes=64
            )
            nc.vector.tensor_tensor(
                out=grouped[(i, c)][:].rearrange("q t m b j -> q m b j t"),
                in0=x_raw[i][:].rearrange("q b j (m c t) -> q c m b j t", c=STEPS, t=STEP)[:, c],
                in1=pe[c][:].unsqueeze(2).to_broadcast([P, ROWS, PAIR, PACK, STEP]),
                op=ALU.add,
            )

        def quantise_tokens(i, c, parts=1):
            count = STEP // parts
            for part in range(parts):
                span = slice(STEP * c + count * part, STEP * c + count * (part + 1))
                nc.vector.quantize_mx(
                    out=codes[i][:, span, :].rearrange("q t m -> q (t m)").bitcast(FP8X4),
                    scales=scales[i][:, span, :].rearrange("q t m -> q (t m)"),
                    in_=grouped[(i, c)][:, count * part : count * (part + 1), :, :, :].rearrange(
                        "q t m b j -> q (t m b j)"
                    ),
                )

        pieces = [
            (0, 0, 1, 0, 1), (0, 1, 1, 0, 1), (0, 2, 1, 0, 1), (0, 3, 1, 0, 1), (0, 4, 1, 0, 2), (0, 5, 1, 0, 2), (0, 0, 1, 1, 3), (0, 1, 1, 1, 4), (0, 2, 1, 1, 4), (0, 3, 1, 1, 4), (0, 0, 1, 3, 4), (0, 4, 2, 2, 4), (1, 0, 1, 0, 4), (1, 1, 1, 0, 4), (1, 2, 2, 0, 4), (1, 4, 2, 0, 4),
        ]
        staged = {}
        place = 0
        for piece in pieces:
            i, s0, n, c0, c1 = piece
            size = SIXTH_HEADS * n * STEP * (c1 - c0) * HEAD_DIM * 4
            if place + size > STAGING:
                place = 0
            for s in range(s0, s0 + n):
                for c in range(c0, c1):
                    staged[(i, s, c)] = (place, piece)
            place += size
        stage = {}

        def project(i, s, first, end, on_vector=()):
            cols = slice(SIXTH_COLS * s, SIXTH_COLS * (s + 1))
            for k, t in enumerate(range(STEP * first, STEP * end, 2)):
                offset, piece = staged[(i, s, t // STEP)]
                s0, n, c0, c1 = piece[1:]
                if piece not in stage:
                    stage[piece] = staging.tile(
                        [P, SIXTH_HEADS * n, STEP * (c1 - c0), HEAD_DIM], F32,
                        name="stage%d%d%d" % (i, s0, c0), offset=offset,
                    )
                acc = psum.tile([P, 2, SIXTH_COLS], F32, tag="bank")
                for r in range(2):
                    nc.tensor.matmul_mx(
                        out=acc[:, r, :],
                        lhsT=codes[i][:, t + r, :].bitcast(FP8X4),
                        lhsT_scale=scales[i][:, t + r, :],
                        rhs=w_codes[:, cols].bitcast(FP8X4),
                        rhs_scale=w_scales[:, cols],
                        start=True,
                        stop=True,
                    )
                src = acc[:].rearrange("m r (h d) -> m r h d", d=HEAD_DIM)
                heads = slice(SIXTH_HEADS * (s - s0), SIXTH_HEADS * (s - s0 + 1))
                slots = slice(t - STEP * c0, t - STEP * c0 + 2)
                dst = stage[piece][:, heads, slots, :].rearrange("m h r d -> m r h d")
                if k in on_vector:
                    nc.vector.tensor_copy(out=dst, in_=src)
                else:
                    nc.scalar.copy(out=dst, in_=src)

        def store(i, s, c):
            piece = staged[(i, s, c)][1]
            s0, n, c0, c1 = piece[1:]
            heads = slice(SIXTH_HEADS * (s0 % 2), SIXTH_HEADS * (s0 % 2 + n))
            span = slice(HEAD_DIM * STEP * c0, HEAD_DIM * STEP * c1)
            for b in range(PAIR):
                nc.sync.dma_start(
                    out=outs[s0 // 2][PAIR * i + b].rearrange("h (m t) d -> m h (t d)", t=RUN)[:, heads, span],
                    in_=stage[piece][:].rearrange("p h t d -> p h (t d)")[b::PAIR],
                )

        def keep_warm(rows):
            for k in range(2):
                idle = psum.tile([P, OUT_COLS], F32, name="idle", tag="bank")
                nc.tensor.matmul(idle[:], rows[:, 0:P], rows[:, 0:OUT_COLS], start=True, stop=True)

        def sums(i, c):
            return grouped[(i, c)][:].rearrange("q t m b j -> q (t m b j)")

        flip_w(0)
        make_back((lambda: regroup_half(0, 0, True), lambda: regroup_half(0, 1, True)))
        make_first_table()
        quantise_w(0)
        make_bend()
        make_twice()
        make_second_table()
        add_table(0, 0)
        flip_w(1)
        regroup_w(1)
        flip_w(2)
        regroup_w(2)
        quantise_tokens(0, 0, 2)
        quantise_w(1)
        for s in range(2):
            project(0, s, 0, 1)
            store(0, s, 0)
        add_table(0, 1)
        for s in range(2, 4):
            project(0, s, 0, 1)
            store(0, s, 0)
        quantise_w(2)
        quantise_tokens(0, 1)
        make_next_table(2)
        add_table(0, 2)
        for s in range(4, 6):
            project(0, s, 0, 2)
            store(0, s, 0)
        make_next_table(3)
        quantise_tokens(0, 2)
        add_table(0, 3)
        project(0, 0, 1, 3)
        store(0, 0, 1)
        project(0, 1, 1, 3)
        quantise_tokens(0, 3)
        project(0, 1, 3, 4, (1,))
        store(0, 1, 1)
        add_table(1, 0)
        project(0, 2, 1, 4, (5,))
        store(0, 2, 1)
        quantise_tokens(1, 0)
        add_table(1, 1)
        project(0, 3, 1, 4)
        store(0, 3, 1)
        project(0, 0, 3, 4, (1,))
        store(0, 0, 3)
        quantise_tokens(1, 1)
        add_table(1, 2)
        quantise_tokens(1, 2)
        add_table(1, 3)
        for s in range(4, 6):
            project(0, s, 2, 4)
        store(0, 4, 2)
        project(1, 0, 0, 3)
        quantise_tokens(1, 3, 2)
        keep_warm(sums(1, 3))
        project(1, 0, 3, 4, (1,))
        store(1, 0, 0)

        project(1, 1, 0, STEPS, range(1, RUN // 2, 2))
        store(1, 1, 0)
        for s in range(2, SIXTHS, 2):
            project(1, s, 0, STEPS, range(1, RUN // 2, 2))
            project(1, s + 1, 0, STEPS, range(1, RUN // 2, 2))
            store(1, s, 0)
